import numpy as np
import ml_dtypes


def mxq(x, axis, fmt="e4m3"):
    dtype, down = {"e4m3": (ml_dtypes.float8_e4m3fn, 7), "e5m2": (ml_dtypes.float8_e5m2, 14)}[fmt]
    v = np.moveaxis(np.asarray(x, np.float32).astype(ml_dtypes.bfloat16).astype(np.float64), axis, -1)
    blocks = v.reshape(v.shape[:-1] + (-1, 32))
    amax = np.abs(blocks).max(-1, keepdims=True)
    byte = np.maximum(np.where(amax > 0, np.frexp(amax)[1] - 1 + 127, 0) - down, 1)
    scale = np.exp2(byte - 127.0)
    codes = (blocks / scale).astype(np.float32).astype(dtype).astype(np.float64)
    return np.moveaxis((codes * scale).reshape(v.shape), -1, axis)


WIDE = False


def mx_kscale(k):
    if not WIDE:
        return np.ones(k)
    levels = np.array([10, -10, 5, -5, 0])
    a = np.random.permutation(np.resize(levels, k // 512 * 4)).reshape(k // 512, 4)
    idx = np.arange(k)
    return np.exp2(a[idx // 512, idx % 128 // 32])


BF16 = ml_dtypes.bfloat16


def bf(x):
    return np.asarray(x, np.float32).astype(BF16)


def f64(x):
    return np.asarray(x).astype(np.float64)


E2M1 = np.array([0.0, 0.5, 1.0, 1.5, 2.0, 3.0, 4.0, 6.0, -0.0, -0.5, -1.0, -1.5, -2.0, -3.0, -4.0, -6.0])


def pack_weight(w, fmt):
    k, n = w.shape
    w = f64(bf(w)).reshape(k // 32, 32, n)
    amax = np.abs(w).max(1)
    if fmt == "e4m3":
        byte = np.frexp(amax)[1] - 1 + 127 - 7
    else:
        mant, ex = np.frexp(amax / 6.0)
        byte = np.where(mant > 0.5, ex, ex - 1) + 127
    byte = np.clip(np.where(amax > 0, byte, 1), 1, 254)
    scaled = (w * np.exp2(127.0 - byte)[:, None, :]).reshape(k, n).astype(np.float32)
    by_word = np.ascontiguousarray(scaled.reshape(k // 512, 128, 4, n).transpose(0, 1, 3, 2))
    if fmt == "e4m3":
        words = by_word.astype(ml_dtypes.float8_e4m3fn).view(np.uint8)
    else:
        c = by_word.astype(ml_dtypes.float4_e2m1fn).view(np.uint8) & 0xF
        words = c[..., 0::2] | (c[..., 1::2] << 4)
    return np.ascontiguousarray(words), np.ascontiguousarray(byte.astype(np.uint8).reshape(k // 512, 16, n))


def unpack_weight(words, scales, fmt):
    g, p, n, _ = words.shape
    if fmt == "e4m3":
        vals = np.ascontiguousarray(words).view(ml_dtypes.float8_e4m3fn).astype(np.float64)
    else:
        nib = np.empty((g, p, n, 4), np.uint8)
        nib[..., 0::2] = words & 0xF
        nib[..., 1::2] = words >> 4
        vals = E2M1[nib]
    vals = vals * np.repeat(np.exp2(scales.astype(np.float64) - 127.0), 8, axis=1)[..., None]
    return vals.transpose(0, 1, 3, 2).reshape(g * 512, n)

def pack4(w):
    words, scales = pack_weight(w, "e2m1")
    return words.reshape(words.shape[0], 128, -1), scales


def unpack4(words, scales):
    return unpack_weight(words.reshape(words.shape[0], 128, -1, 2), scales, "e2m1")


IN_C, OUT_C, N, ND = 8192, 1024, 512, 2


def sigmoid(v):
    return 1.0 / (1.0 + np.exp(-v))


def setup_inputs():
    s, t = mx_kscale(IN_C), mx_kscale(OUT_C)
    rn = np.random.standard_normal
    x = bf(rn((IN_C, N)) * s[:, None])
    h_prev_dim0 = bf(rn((OUT_C, N)) * t[:, None])
    h_prev_dim1 = bf(rn((OUT_C, N)) * t[:, None])
    ct0 = bf(rn((OUT_C, N)) * 0.65)
    ct1 = bf(rn((OUT_C, N)) * 0.65)
    w_io = rn((OUT_C, IN_C)) * 0.7 / np.sqrt(IN_C) / s[None, :]
    w_ho = rn((OUT_C, OUT_C)) * 0.7 / np.sqrt(OUT_C) / t[None, :]
    b_o = bf(rn((OUT_C, 1)) * 0.5)
    weighted_sum = bf(0.4 + 0.5 * np.random.random(ND))
    w_io_words, w_io_scales = pack4(np.ascontiguousarray(w_io.T))
    w_ho_words, w_ho_scales = pack4(np.ascontiguousarray(w_ho.T))
    return {"x": x,
            "h_prev_dim0": h_prev_dim0,
            "h_prev_dim1": h_prev_dim1,
            "ct0": ct0,
            "ct1": ct1,
            "w_io_words": w_io_words,
            "w_io_scales": w_io_scales,
            "w_ho_words": w_ho_words,
            "w_ho_scales": w_ho_scales,
            "b_o": b_o,
            "weighted_sum": weighted_sum}


def reference(x, h_prev_dim0, h_prev_dim1, ct0, ct1, w_io_words, w_io_scales, w_ho_words, w_ho_scales, b_o, weighted_sum):
    xo = unpack4(w_io_words, w_io_scales).T @ mxq(f64(x), 0, "e4m3")
    who = unpack4(w_ho_words, w_ho_scales).T
    ws = f64(weighted_sum)

    def hidden(h_prev, c):
        o = sigmoid(xo + (who @ mxq(f64(h_prev), 0, "e4m3")) + f64(b_o))
        return o * np.tanh(f64(c))

    ht0 = hidden(h_prev_dim0, ct0)
    ht1 = hidden(h_prev_dim1, ct1)
    return ht0 * ws[0] + ht1 * ws[1]

@@ -1,0 +1,235 @@
+from contextlib import ExitStack
+
+import concourse.mybir as mybir
+
+F32 = mybir.dt.float32
+BF16 = mybir.dt.bfloat16
+I32 = mybir.dt.int32
+U32 = mybir.dt.uint32
+U8 = mybir.dt.uint8
+FP8X4 = mybir.dt.float8_e4m3fn_x4
+FP4X4 = mybir.dt.float4_e2m1fn_x4
+ACT = mybir.ActivationFunctionType
+ALU = mybir.AluOpType
+
+P = 128
+PACK = 4
+K_PASS = P * PACK
+IN_C, OUT_C, N = 8192, 1024, 512
+X_PASSES = IN_C // K_PASS
+H_PASSES = OUT_C // K_PASS
+M_TILES = OUT_C // P
+DIRS = 2
+WORD_BYTES = 2
+TILE_WORD_BYTES = P * WORD_BYTES
+
+STREAMED_TILES = 6
+PASSES_PER_LOAD = 4
+RAW_BUFS = 8
+
+FLOPS = 2 * OUT_C * N * (IN_C + DIRS * OUT_C)
+
+
+def load_scale_rows(nc, planes, scales, passes):
+    for q in range(8):
+        first = 32 * (q // 4) + q % 4
+        nc.sync.dma_start(
+            out=planes[first : P : 64, passes, :].bitcast(I32),
+            in_=scales[passes, q : 16 : 8, :].rearrange("g q n -> q g n").bitcast(I32),
+        )
+
+
+def load_words(nc, words_sb, words, passes, columns):
+    nc.sync.dma_start(
+        out=words_sb[:, passes, columns].bitcast(I32),
+        in_=words[passes, :, columns].rearrange("g p b -> p g b").bitcast(I32),
+    )
+
+
+def tile_mdlstmcellweights_pb_k_kernel(
+    tc,
+    x,
+    h_prev_dim0,
+    h_prev_dim1,
+    ct0,
+    ct1,
+    w_io_words,
+    w_io_scales,
+    w_ho_words,
+    w_ho_scales,
+    b_o,
+    weighted_sum,
+    out,
+):
+    nc = tc.nc
+    h_prev = [h_prev_dim0, h_prev_dim1]
+    cell = [ct0, ct1]
+
+    with ExitStack() as stack:
+        keep = stack.enter_context(tc.tile_pool(name="keep", bufs=1))
+        raw_pool = stack.enter_context(tc.tile_pool(name="raw", bufs=RAW_BUFS))
+        grouped_pool = stack.enter_context(tc.tile_pool(name="grouped", bufs=3))
+        work = stack.enter_context(tc.tile_pool(name="work", bufs=3))
+        banks = stack.enter_context(tc.psum_pool(name="banks", bufs=8))
+
+        io_words = keep.tile([P, X_PASSES, OUT_C * WORD_BYTES], U8, align_bytes=64)
+        io_planes = keep.tile([P, X_PASSES, OUT_C], U8, align_bytes=64)
+        ho_words = keep.tile([P, H_PASSES, OUT_C * WORD_BYTES], U8, align_bytes=64)
+        ho_planes = keep.tile([P, H_PASSES, OUT_C], U8, align_bytes=64)
+        x_codes = keep.tile([P, X_PASSES, N], U32, align_bytes=64)
+        x_planes = keep.tile([P, X_PASSES, N], U8, align_bytes=64)
+        h_codes = keep.tile([P, DIRS, H_PASSES, N], U32, align_bytes=64)
+        h_planes = keep.tile([P, DIRS, H_PASSES, N], U8, align_bytes=64)
+        cell_sb = keep.tile([P, M_TILES, DIRS, N], BF16)
+        bias_bf = keep.tile([P, M_TILES], BF16)
+        mix_bf = keep.tile([P, DIRS], BF16)
+        bias = keep.tile([P, M_TILES], F32)
+        mix = keep.tile([P, DIRS], F32)
+        warm = keep.tile([P, 1], F32)
+
+        nc.vector.memset(warm[:], 0.0)
+        nc.scalar.activation(out=warm[:], in_=warm[:], func=ACT.Sigmoid)
+
+        nc.vector.memset(io_planes[:].rearrange("p g n -> p (g n)").bitcast(I32), 0)
+        nc.vector.memset(ho_planes[:].rearrange("p g n -> p (g n)").bitcast(I32), 0)
+
+        def load_pass(rows):
+            raw = raw_pool.tile([P, PACK, N], BF16, name="raw")
+            nc.sync.dma_start(out=raw[:], in_=rows.rearrange("(p t) n -> p t n", t=PACK))
+            return raw
+
+        def load_x(g):
+            return load_pass(x[g * K_PASS : (g + 1) * K_PASS, :])
+
+        def load_cell(m0, m1):
+            for d in range(DIRS):
+                nc.sync.dma_start(
+                    out=cell_sb[:, m0:m1, d, :],
+                    in_=cell[d][m0 * P : m1 * P, :].rearrange("(m p) n -> p m n", p=P),
+                )
+
+        streamed_columns = slice(0, STREAMED_TILES * TILE_WORD_BYTES)
+        late_columns = slice(STREAMED_TILES * TILE_WORD_BYTES, M_TILES * TILE_WORD_BYTES)
+        half = X_PASSES // 2
+
+        with nc.allow_non_contiguous_dma(reason="b_o: one 2-byte element for each partition and tile"):
+            nc.scalar.dma_start(out=bias_bf[:], in_=b_o.rearrange("(m p) o -> p (m o)", p=P))
+        nc.scalar.dma_start(out=mix_bf[:], in_=weighted_sum.partition_broadcast(P))
+
+        x_raw = [load_x(0), load_x(1)]
+        for g0 in range(0, half, PASSES_PER_LOAD):
+            load_scale_rows(nc, io_planes, w_io_scales, slice(g0, g0 + PASSES_PER_LOAD))
+        for g0 in range(0, half, PASSES_PER_LOAD):
+            load_words(nc, io_words, w_io_words, slice(g0, g0 + PASSES_PER_LOAD), streamed_columns)
+            x_raw.extend([load_x(g) for g in range(max(g0, 2), g0 + PASSES_PER_LOAD)])
+        h_raw = [[load_pass(h_prev[d][c * K_PASS : (c + 1) * K_PASS, :]) for c in range(H_PASSES)] for d in range(DIRS)]
+        load_scale_rows(nc, ho_planes, w_ho_scales, slice(0, H_PASSES))
+        for g0 in range(half, X_PASSES, PASSES_PER_LOAD):
+            load_scale_rows(nc, io_planes, w_io_scales, slice(g0, g0 + PASSES_PER_LOAD))
+        load_words(nc, ho_words, w_ho_words, slice(0, H_PASSES), slice(0, M_TILES * TILE_WORD_BYTES))
+        for g0 in range(half, X_PASSES, PASSES_PER_LOAD):
+            load_words(nc, io_words, w_io_words, slice(g0, g0 + PASSES_PER_LOAD), streamed_columns)
+            x_raw.extend([load_x(g) for g in range(g0, g0 + PASSES_PER_LOAD)])
+        load_cell(0, M_TILES // 2)
+        load_words(nc, io_words, w_io_words, slice(0, X_PASSES), late_columns)
+        load_cell(M_TILES // 2, M_TILES)
+
+        nc.vector.tensor_copy(out=bias[:], in_=bias_bf[:])
+        nc.vector.tensor_copy(out=mix[:], in_=mix_bf[:])
+
+        def quantise_pass(raw, codes, plane):
+            grouped = grouped_pool.tile([P, N, PACK], BF16, name="grouped", align_bytes=64)
+            nc.vector.tensor_copy(
+                out=grouped[:, : N // 2, :].rearrange("p (c i) t -> p c t i", i=4),
+                in_=raw[:, :, : N // 2].rearrange("p t (c i) -> p c t i", i=4),
+            )
+            nc.scalar.copy(
+                out=grouped[:, N // 2 :, :].rearrange("p (c i) t -> p c t i", i=4),
+                in_=raw[:, :, N // 2 :].rearrange("p t (c i) -> p c t i", i=4),
+            )
+            nc.vector.quantize_mx(
+                out=codes.bitcast(FP8X4),
+                scales=plane,
+                in_=grouped[:].rearrange("p n t -> p (n t)"),
+            )
+
+        def new_bank():
+            return banks.tile([P, N], F32, name="bank")
+
+        def weight_pass(acc, words_sb, planes, g, m, codes, plane, start, stop):
+            nc.tensor.matmul_mx(
+                out=acc[:],
+                lhsT=words_sb[:, g, m * TILE_WORD_BYTES : (m + 1) * TILE_WORD_BYTES].bitcast(FP4X4),
+                lhsT_scale=planes[:, g, m * P : (m + 1) * P],
+                rhs=codes.bitcast(FP8X4),
+                rhs_scale=plane,
+                start=start,
+                stop=stop,
+            )
+
+        def x_pass(acc, g, m):
+            weight_pass(
+                acc, io_words, io_planes, g, m, x_codes[:, g, :], x_planes[:, g, :],
+                start=(g == 0), stop=(g == X_PASSES - 1),
+            )
+
+        def hidden_products(m):
+            products = []
+            for d in range(DIRS):
+                acc = new_bank()
+                for c in range(H_PASSES):
+                    weight_pass(
+                        acc, ho_words, ho_planes, c, m, h_codes[:, d, c, :], h_planes[:, d, c, :],
+                        start=(c == 0), stop=(c == H_PASSES - 1),
+                    )
+                products.append(acc)
+            return products
+
+        def finish_tile(m, x_product, h_products):
+            x_sum = work.tile([P, N], F32, name="x_sum")
+            nc.scalar.copy(out=x_sum[:], in_=x_product[:])
+            gate = work.tile([P, DIRS, N], F32, name="gate")
+            for d in range(DIRS):
+                nc.vector.tensor_tensor(out=gate[:, d, :], in0=h_products[d][:], in1=x_sum[:], op=ALU.add)
+            both = gate[:].rearrange("p d n -> p (d n)")
+            nc.scalar.activation(out=both, in_=both, func=ACT.Sigmoid, bias=bias[:, m : m + 1])
+            tanh_c = work.tile([P, DIRS, N], F32, name="tanh_c")
+            nc.scalar.activation(
+                out=tanh_c[:].rearrange("p d n -> p (d n)"),
+                in_=cell_sb[:, m, :, :].rearrange("p d n -> p (d n)"),
+                func=ACT.Tanh,
+            )
+            for d in range(DIRS):
+                nc.vector.scalar_tensor_tensor(
+                    out=gate[:, d, :], in0=gate[:, d, :], scalar=mix[:, d : d + 1], in1=tanh_c[:, d, :],
+                    op0=ALU.mult, op1=ALU.mult,
+                )
+            result = work.tile([P, N], F32, name="result")
+            nc.vector.tensor_tensor(out=result[:], in0=gate[:, 0, :], in1=gate[:, 1, :], op=ALU.add)
+            nc.sync.dma_start(out=out[m * P : (m + 1) * P, :], in_=result[:])
+
+        x_products = [new_bank() for m in range(STREAMED_TILES)]
+
+        def stream_x(g):
+            quantise_pass(x_raw[g], x_codes[:, g, :], x_planes[:, g, :])
+            for m in range(STREAMED_TILES):
+                x_pass(x_products[m], g, m)
+
+        for g in range(half):
+            stream_x(g)
+        for d in range(DIRS):
+            for c in range(H_PASSES):
+                quantise_pass(h_raw[d][c], h_codes[:, d, c, :], h_planes[:, d, c, :])
+        first_h_products = hidden_products(0)
+        for g in range(half, X_PASSES):
+            stream_x(g)
+
+        for m in range(M_TILES):
+            if m < STREAMED_TILES:
+                x_product = x_products[m]
+            else:
+                x_product = new_bank()
+                for g in range(X_PASSES):
+                    x_pass(x_product, g, m)
+            h_products = first_h_products if m == 0 else hidden_products(m)
+            finish_tile(m, x_product, h_products)

@@ -24,6 +24,7 @@ WORD_BYTES = 2
 TILE_WORD_BYTES = P * WORD_BYTES
 
 STREAMED_TILES = 6
+LATE_TILES = M_TILES - STREAMED_TILES
 PASSES_PER_LOAD = 4
 RAW_BUFS = 8
 
@@ -41,7 +42,7 @@ def load_scale_rows(nc, planes, scales, passes):
 
 def load_words(nc, words_sb, words, passes, columns):
     nc.sync.dma_start(
-        out=words_sb[:, passes, columns].bitcast(I32),
+        out=words_sb[:, passes, :].bitcast(I32),
         in_=words[passes, :, columns].rearrange("g p b -> p g b").bitcast(I32),
     )
 
@@ -72,7 +73,8 @@ def tile_mdlstmcellweights_pb_k_kernel(
         work = stack.enter_context(tc.tile_pool(name="work", bufs=3))
         banks = stack.enter_context(tc.psum_pool(name="banks", bufs=8))
 
-        io_words = keep.tile([P, X_PASSES, OUT_C * WORD_BYTES], U8, align_bytes=64)
+        streamed_words = keep.tile([P, X_PASSES, STREAMED_TILES * TILE_WORD_BYTES], U8, align_bytes=64)
+        late_words = keep.tile([P, X_PASSES, LATE_TILES * TILE_WORD_BYTES], U8, align_bytes=64)
         io_planes = keep.tile([P, X_PASSES, OUT_C], U8, align_bytes=64)
         ho_words = keep.tile([P, H_PASSES, OUT_C * WORD_BYTES], U8, align_bytes=64)
         ho_planes = keep.tile([P, H_PASSES, OUT_C], U8, align_bytes=64)
@@ -81,10 +83,8 @@ def tile_mdlstmcellweights_pb_k_kernel(
         h_codes = keep.tile([P, DIRS, H_PASSES, N], U32, align_bytes=64)
         h_planes = keep.tile([P, DIRS, H_PASSES, N], U8, align_bytes=64)
         cell_sb = keep.tile([P, M_TILES, DIRS, N], BF16)
-        bias_bf = keep.tile([P, M_TILES], BF16)
-        mix_bf = keep.tile([P, DIRS], BF16)
-        bias = keep.tile([P, M_TILES], F32)
-        mix = keep.tile([P, DIRS], F32)
+        bias = keep.tile([P, M_TILES], BF16)
+        mix = keep.tile([P, DIRS], BF16)
         warm = keep.tile([P, 1], F32)
 
         nc.vector.memset(warm[:], 0.0)
@@ -113,14 +113,14 @@ def tile_mdlstmcellweights_pb_k_kernel(
         half = X_PASSES // 2
 
         with nc.allow_non_contiguous_dma(reason="b_o: one 2-byte element for each partition and tile"):
-            nc.scalar.dma_start(out=bias_bf[:], in_=b_o.rearrange("(m p) o -> p (m o)", p=P))
-        nc.scalar.dma_start(out=mix_bf[:], in_=weighted_sum.partition_broadcast(P))
+            nc.scalar.dma_start(out=bias[:], in_=b_o.rearrange("(m p) o -> p (m o)", p=P))
+        nc.scalar.dma_start(out=mix[:], in_=weighted_sum.partition_broadcast(P))
 
         x_raw = [load_x(0), load_x(1)]
         for g0 in range(0, half, PASSES_PER_LOAD):
             load_scale_rows(nc, io_planes, w_io_scales, slice(g0, g0 + PASSES_PER_LOAD))
         for g0 in range(0, half, PASSES_PER_LOAD):
-            load_words(nc, io_words, w_io_words, slice(g0, g0 + PASSES_PER_LOAD), streamed_columns)
+            load_words(nc, streamed_words, w_io_words, slice(g0, g0 + PASSES_PER_LOAD), streamed_columns)
             x_raw.extend([load_x(g) for g in range(max(g0, 2), g0 + PASSES_PER_LOAD)])
         h_raw = [[load_pass(h_prev[d][c * K_PASS : (c + 1) * K_PASS, :]) for c in range(H_PASSES)] for d in range(DIRS)]
         load_scale_rows(nc, ho_planes, w_ho_scales, slice(0, H_PASSES))
@@ -128,14 +128,11 @@ def tile_mdlstmcellweights_pb_k_kernel(
             load_scale_rows(nc, io_planes, w_io_scales, slice(g0, g0 + PASSES_PER_LOAD))
         load_words(nc, ho_words, w_ho_words, slice(0, H_PASSES), slice(0, M_TILES * TILE_WORD_BYTES))
         for g0 in range(half, X_PASSES, PASSES_PER_LOAD):
-            load_words(nc, io_words, w_io_words, slice(g0, g0 + PASSES_PER_LOAD), streamed_columns)
+            load_words(nc, streamed_words, w_io_words, slice(g0, g0 + PASSES_PER_LOAD), streamed_columns)
             x_raw.extend([load_x(g) for g in range(g0, g0 + PASSES_PER_LOAD)])
         load_cell(0, M_TILES // 2)
-        load_words(nc, io_words, w_io_words, slice(0, X_PASSES), late_columns)
+        load_words(nc, late_words, w_io_words, slice(0, X_PASSES), late_columns)
         load_cell(M_TILES // 2, M_TILES)
-
-        nc.vector.tensor_copy(out=bias[:], in_=bias_bf[:])
-        nc.vector.tensor_copy(out=mix[:], in_=mix_bf[:])
 
         def quantise_pass(raw, codes, plane):
             grouped = grouped_pool.tile([P, N, PACK], BF16, name="grouped", align_bytes=64)
@@ -156,10 +153,10 @@ def tile_mdlstmcellweights_pb_k_kernel(
         def new_bank():
             return banks.tile([P, N], F32, name="bank")
 
-        def weight_pass(acc, words_sb, planes, g, m, codes, plane, start, stop):
+        def weight_pass(acc, words_sb, word_tile, planes, g, m, codes, plane, start, stop):
             nc.tensor.matmul_mx(
                 out=acc[:],
-                lhsT=words_sb[:, g, m * TILE_WORD_BYTES : (m + 1) * TILE_WORD_BYTES].bitcast(FP4X4),
+                lhsT=words_sb[:, g, word_tile * TILE_WORD_BYTES : (word_tile + 1) * TILE_WORD_BYTES].bitcast(FP4X4),
                 lhsT_scale=planes[:, g, m * P : (m + 1) * P],
                 rhs=codes.bitcast(FP8X4),
                 rhs_scale=plane,
@@ -168,8 +165,12 @@ def tile_mdlstmcellweights_pb_k_kernel(
             )
 
         def x_pass(acc, g, m):
+            if m < STREAMED_TILES:
+                words_sb, word_tile = streamed_words, m
+            else:
+                words_sb, word_tile = late_words, m - STREAMED_TILES
             weight_pass(
-                acc, io_words, io_planes, g, m, x_codes[:, g, :], x_planes[:, g, :],
+                acc, words_sb, word_tile, io_planes, g, m, x_codes[:, g, :], x_planes[:, g, :],
                 start=(g == 0), stop=(g == X_PASSES - 1),
             )
 
@@ -179,7 +180,7 @@ def tile_mdlstmcellweights_pb_k_kernel(
                 acc = new_bank()
                 for c in range(H_PASSES):
                     weight_pass(
-                        acc, ho_words, ho_planes, c, m, h_codes[:, d, c, :], h_planes[:, d, c, :],
+                        acc, ho_words, m, ho_planes, c, m, h_codes[:, d, c, :], h_planes[:, d, c, :],
                         start=(c == 0), stop=(c == H_PASSES - 1),
                     )
                 products.append(acc)

@@ -20,23 +20,26 @@ X_PASSES = IN_C // K_PASS
 H_PASSES = OUT_C // K_PASS
 M_TILES = OUT_C // P
 DIRS = 2
-WORD_BYTES = 2
-TILE_WORD_BYTES = P * WORD_BYTES
+TILE_WORD_BYTES = P * 2
+SCALE_ROWS = K_PASS // 32
 
+PSUM_BANKS = 8
 STREAMED_TILES = 6
 LATE_TILES = M_TILES - STREAMED_TILES
-PASSES_PER_LOAD = 4
+SCALE_GROUP = 4
+H_AFTER = 7
+LATE_AHEAD = 4
 RAW_BUFS = 8
 
 FLOPS = 2 * OUT_C * N * (IN_C + DIRS * OUT_C)
 
 
-def load_scale_rows(nc, planes, scales, passes):
-    for q in range(8):
-        first = 32 * (q // 4) + q % 4
+def load_scale_rows(nc, planes, scales, passes, rows):
+    for q in rows:
+        partition = 32 * (q // 4) + q % 4
         nc.sync.dma_start(
-            out=planes[first : P : 64, passes, :].bitcast(I32),
-            in_=scales[passes, q : 16 : 8, :].rearrange("g q n -> q g n").bitcast(I32),
+            out=planes[partition : P : 64, passes, :].bitcast(I32),
+            in_=scales[passes, q : SCALE_ROWS : 8, :].rearrange("g q n -> q g n").bitcast(I32),
         )
 
 
@@ -67,16 +70,17 @@ def tile_mdlstmcellweights_pb_k_kernel(
     cell = [ct0, ct1]
 
     with ExitStack() as stack:
+        stack.enter_context(tc.manual_schedule())
         keep = stack.enter_context(tc.tile_pool(name="keep", bufs=1))
         raw_pool = stack.enter_context(tc.tile_pool(name="raw", bufs=RAW_BUFS))
         grouped_pool = stack.enter_context(tc.tile_pool(name="grouped", bufs=3))
         work = stack.enter_context(tc.tile_pool(name="work", bufs=3))
-        banks = stack.enter_context(tc.psum_pool(name="banks", bufs=8))
+        banks = stack.enter_context(tc.psum_pool(name="banks", bufs=PSUM_BANKS))
 
         streamed_words = keep.tile([P, X_PASSES, STREAMED_TILES * TILE_WORD_BYTES], U8, align_bytes=64)
         late_words = keep.tile([P, X_PASSES, LATE_TILES * TILE_WORD_BYTES], U8, align_bytes=64)
         io_planes = keep.tile([P, X_PASSES, OUT_C], U8, align_bytes=64)
-        ho_words = keep.tile([P, H_PASSES, OUT_C * WORD_BYTES], U8, align_bytes=64)
+        ho_words = keep.tile([P, H_PASSES, M_TILES * TILE_WORD_BYTES], U8, align_bytes=64)
         ho_planes = keep.tile([P, H_PASSES, OUT_C], U8, align_bytes=64)
         x_codes = keep.tile([P, X_PASSES, N], U32, align_bytes=64)
         x_planes = keep.tile([P, X_PASSES, N], U8, align_bytes=64)
@@ -90,7 +94,9 @@ def tile_mdlstmcellweights_pb_k_kernel(
         nc.vector.memset(warm[:], 0.0)
         nc.scalar.activation(out=warm[:], in_=warm[:], func=ACT.Sigmoid)
 
-        nc.vector.memset(io_planes[:].rearrange("p g n -> p (g n)").bitcast(I32), 0)
+        for g0 in range(0, X_PASSES, SCALE_GROUP):
+            group = io_planes[:, g0 : g0 + SCALE_GROUP, :]
+            nc.vector.memset(group.rearrange("p g n -> p (g n)").bitcast(I32), 0)
         nc.vector.memset(ho_planes[:].rearrange("p g n -> p (g n)").bitcast(I32), 0)
 
         def load_pass(rows):
@@ -98,8 +104,8 @@ def tile_mdlstmcellweights_pb_k_kernel(
             nc.sync.dma_start(out=raw[:], in_=rows.rearrange("(p t) n -> p t n", t=PACK))
             return raw
 
-        def load_x(g):
-            return load_pass(x[g * K_PASS : (g + 1) * K_PASS, :])
+        def load_streamed_words(g):
+            load_words(nc, streamed_words, w_io_words, slice(g, g + 1), slice(0, STREAMED_TILES * TILE_WORD_BYTES))
 
         def load_cell(m0, m1):
             for d in range(DIRS):
@@ -108,50 +114,41 @@ def tile_mdlstmcellweights_pb_k_kernel(
                     in_=cell[d][m0 * P : m1 * P, :].rearrange("(m p) n -> p m n", p=P),
                 )
 
-        streamed_columns = slice(0, STREAMED_TILES * TILE_WORD_BYTES)
-        late_columns = slice(STREAMED_TILES * TILE_WORD_BYTES, M_TILES * TILE_WORD_BYTES)
-        half = X_PASSES // 2
-
         with nc.allow_non_contiguous_dma(reason="b_o: one 2-byte element for each partition and tile"):
             nc.scalar.dma_start(out=bias[:], in_=b_o.rearrange("(m p) o -> p (m o)", p=P))
         nc.scalar.dma_start(out=mix[:], in_=weighted_sum.partition_broadcast(P))
 
-        x_raw = [load_x(0), load_x(1)]
-        for g0 in range(0, half, PASSES_PER_LOAD):
-            load_scale_rows(nc, io_planes, w_io_scales, slice(g0, g0 + PASSES_PER_LOAD))
-        for g0 in range(0, half, PASSES_PER_LOAD):
-            load_words(nc, streamed_words, w_io_words, slice(g0, g0 + PASSES_PER_LOAD), streamed_columns)
-            x_raw.extend([load_x(g) for g in range(max(g0, 2), g0 + PASSES_PER_LOAD)])
-        h_raw = [[load_pass(h_prev[d][c * K_PASS : (c + 1) * K_PASS, :]) for c in range(H_PASSES)] for d in range(DIRS)]
-        load_scale_rows(nc, ho_planes, w_ho_scales, slice(0, H_PASSES))
-        for g0 in range(half, X_PASSES, PASSES_PER_LOAD):
-            load_scale_rows(nc, io_planes, w_io_scales, slice(g0, g0 + PASSES_PER_LOAD))
-        load_words(nc, ho_words, w_ho_words, slice(0, H_PASSES), slice(0, M_TILES * TILE_WORD_BYTES))
-        for g0 in range(half, X_PASSES, PASSES_PER_LOAD):
-            load_words(nc, streamed_words, w_io_words, slice(g0, g0 + PASSES_PER_LOAD), streamed_columns)
-            x_raw.extend([load_x(g) for g in range(g0, g0 + PASSES_PER_LOAD)])
+        rows_per_pass = SCALE_ROWS // 2 // SCALE_GROUP
+        raw_tiles = []
+        for g in range(X_PASSES):
+            raw_tiles.append(load_pass(x[g * K_PASS : (g + 1) * K_PASS, :]))
+            if g == 0:
+                load_scale_rows(nc, io_planes, w_io_scales, slice(0, SCALE_GROUP), range(SCALE_ROWS // 2))
+                load_streamed_words(0)
+            if g + 1 < X_PASSES:
+                load_streamed_words(g + 1)
+            next_group = (g // SCALE_GROUP + 1) * SCALE_GROUP
+            if next_group < X_PASSES:
+                first_row = (g % SCALE_GROUP) * rows_per_pass
+                load_scale_rows(
+                    nc, io_planes, w_io_scales, slice(next_group, next_group + SCALE_GROUP),
+                    range(first_row, first_row + rows_per_pass),
+                )
+            if g == H_AFTER:
+                for d in range(DIRS):
+                    for c in range(H_PASSES):
+                        raw_tiles.append(load_pass(h_prev[d][c * K_PASS : (c + 1) * K_PASS, :]))
+                        first_row = (d * H_PASSES + c) * rows_per_pass
+                        load_scale_rows(
+                            nc, ho_planes, w_ho_scales, slice(0, H_PASSES), range(first_row, first_row + rows_per_pass)
+                        )
+                load_words(nc, ho_words, w_ho_words, slice(0, H_PASSES), slice(0, M_TILES * TILE_WORD_BYTES))
         load_cell(0, M_TILES // 2)
-        load_words(nc, late_words, w_io_words, slice(0, X_PASSES), late_columns)
+        load_words(
+            nc, late_words, w_io_words, slice(0, X_PASSES),
+            slice(STREAMED_TILES * TILE_WORD_BYTES, M_TILES * TILE_WORD_BYTES),
+        )
         load_cell(M_TILES // 2, M_TILES)
-
-        def quantise_pass(raw, codes, plane):
-            grouped = grouped_pool.tile([P, N, PACK], BF16, name="grouped", align_bytes=64)
-            nc.vector.tensor_copy(
-                out=grouped[:, : N // 2, :].rearrange("p (c i) t -> p c t i", i=4),
-                in_=raw[:, :, : N // 2].rearrange("p t (c i) -> p c t i", i=4),
-            )
-            nc.scalar.copy(
-                out=grouped[:, N // 2 :, :].rearrange("p (c i) t -> p c t i", i=4),
-                in_=raw[:, :, N // 2 :].rearrange("p t (c i) -> p c t i", i=4),
-            )
-            nc.vector.quantize_mx(
-                out=codes.bitcast(FP8X4),
-                scales=plane,
-                in_=grouped[:].rearrange("p n t -> p (n t)"),
-            )
-
-        def new_bank():
-            return banks.tile([P, N], F32, name="bank")
 
         def weight_pass(acc, words_sb, word_tile, planes, g, m, codes, plane, start, stop):
             nc.tensor.matmul_mx(
@@ -164,73 +161,121 @@ def tile_mdlstmcellweights_pb_k_kernel(
                 stop=stop,
             )
 
-        def x_pass(acc, g, m):
+        x_products = {}
+        h_products = {}
+
+        def x_pass(g, m):
             if m < STREAMED_TILES:
                 words_sb, word_tile = streamed_words, m
             else:
                 words_sb, word_tile = late_words, m - STREAMED_TILES
             weight_pass(
-                acc, words_sb, word_tile, io_planes, g, m, x_codes[:, g, :], x_planes[:, g, :],
+                x_products[m], words_sb, word_tile, io_planes, g, m, x_codes[:, g, :], x_planes[:, g, :],
                 start=(g == 0), stop=(g == X_PASSES - 1),
             )
 
+        def late_x_product(m):
+            x_products[m] = banks.tile([P, N], F32, name="bank")
+            for g in range(X_PASSES):
+                x_pass(g, m)
+
         def hidden_products(m):
-            products = []
+            h_products[m] = []
             for d in range(DIRS):
-                acc = new_bank()
+                acc = banks.tile([P, N], F32, name="bank")
                 for c in range(H_PASSES):
                     weight_pass(
                         acc, ho_words, m, ho_planes, c, m, h_codes[:, d, c, :], h_planes[:, d, c, :],
                         start=(c == 0), stop=(c == H_PASSES - 1),
                     )
-                products.append(acc)
-            return products
+                h_products[m].append(acc)
 
-        def finish_tile(m, x_product, h_products):
-            x_sum = work.tile([P, N], F32, name="x_sum")
-            nc.scalar.copy(out=x_sum[:], in_=x_product[:])
-            gate = work.tile([P, DIRS, N], F32, name="gate")
-            for d in range(DIRS):
-                nc.vector.tensor_tensor(out=gate[:, d, :], in0=h_products[d][:], in1=x_sum[:], op=ALU.add)
-            both = gate[:].rearrange("p d n -> p (d n)")
-            nc.scalar.activation(out=both, in_=both, func=ACT.Sigmoid, bias=bias[:, m : m + 1])
-            tanh_c = work.tile([P, DIRS, N], F32, name="tanh_c")
+        targets = [(x_codes[:, g, :], x_planes[:, g, :], g) for g in range(H_AFTER + 1)]
+        targets.extend([(h_codes[:, d, c, :], h_planes[:, d, c, :], None) for d in range(DIRS) for c in range(H_PASSES)])
+        targets.extend([(x_codes[:, g, :], x_planes[:, g, :], g) for g in range(H_AFTER + 1, X_PASSES)])
+        last_h = H_AFTER + DIRS * H_PASSES
+
+        def regroup(raw):
+            grouped = grouped_pool.tile([P, N, PACK], BF16, name="grouped", align_bytes=64)
+            nc.vector.tensor_copy(
+                out=grouped[:, : N // 2, :].rearrange("p (c i) t -> p c t i", i=4),
+                in_=raw[:, :, : N // 2].rearrange("p t (c i) -> p c t i", i=4),
+            )
+            nc.scalar.copy(
+                out=grouped[:, N // 2 :, :].rearrange("p (c i) t -> p c t i", i=4),
+                in_=raw[:, :, N // 2 :].rearrange("p t (c i) -> p c t i", i=4),
+            )
+            return grouped
+
+        for m in range(STREAMED_TILES):
+            x_products[m] = banks.tile([P, N], F32, name="bank")
+
+        grouped_tiles = []
+        for i in range(len(raw_tiles) + 1):
+            if i < len(raw_tiles):
+                grouped_tiles.append(regroup(raw_tiles[i]))
+            if i > 0:
+                codes, plane, g = targets[i - 1]
+                nc.vector.quantize_mx(
+                    out=codes.bitcast(FP8X4),
+                    scales=plane,
+                    in_=grouped_tiles[i - 1][:].rearrange("p n t -> p (n t)"),
+                )
+                if g is not None:
+                    for m in range(STREAMED_TILES):
+                        x_pass(g, m)
+                if i - 1 == last_h:
+                    hidden_products(0)
+
+        x_sums, gates, tanhs = {}, {}, {}
+
+        def tanh_cell(m):
+            tanhs[m] = work.tile([P, DIRS, N], F32, name="tanh_c")
             nc.scalar.activation(
-                out=tanh_c[:].rearrange("p d n -> p (d n)"),
+                out=tanhs[m][:].rearrange("p d n -> p (d n)"),
                 in_=cell_sb[:, m, :, :].rearrange("p d n -> p (d n)"),
                 func=ACT.Tanh,
             )
+
+        def move_x_product(m):
+            x_sums[m] = work.tile([P, N], F32, name="x_sum")
+            nc.scalar.copy(out=x_sums[m][:], in_=x_products[m][:])
+
+        def add_products(m):
+            gates[m] = work.tile([P, DIRS, N], F32, name="gate")
+            for d in range(DIRS):
+                nc.vector.tensor_tensor(out=gates[m][:, d, :], in0=h_products[m][d][:], in1=x_sums[m][:], op=ALU.add)
+
+        def sigmoid(m):
+            both = gates[m][:].rearrange("p d n -> p (d n)")
+            nc.scalar.activation(out=both, in_=both, func=ACT.Sigmoid, bias=bias[:, m : m + 1])
+
+        def mix_and_store(m):
+            gate = gates[m]
             for d in range(DIRS):
                 nc.vector.scalar_tensor_tensor(
-                    out=gate[:, d, :], in0=gate[:, d, :], scalar=mix[:, d : d + 1], in1=tanh_c[:, d, :],
+                    out=gate[:, d, :], in0=gate[:, d, :], scalar=mix[:, d : d + 1], in1=tanhs[m][:, d, :],
                     op0=ALU.mult, op1=ALU.mult,
                 )
             result = work.tile([P, N], F32, name="result")
             nc.vector.tensor_tensor(out=result[:], in0=gate[:, 0, :], in1=gate[:, 1, :], op=ALU.add)
             nc.sync.dma_start(out=out[m * P : (m + 1) * P, :], in_=result[:])
 
-        x_products = [new_bank() for m in range(STREAMED_TILES)]
-
-        def stream_x(g):
-            quantise_pass(x_raw[g], x_codes[:, g, :], x_planes[:, g, :])
-            for m in range(STREAMED_TILES):
-                x_pass(x_products[m], g, m)
-
-        for g in range(half):
-            stream_x(g)
-        for d in range(DIRS):
-            for c in range(H_PASSES):
-                quantise_pass(h_raw[d][c], h_codes[:, d, c, :], h_planes[:, d, c, :])
-        first_h_products = hidden_products(0)
-        for g in range(half, X_PASSES):
-            stream_x(g)
-
+        tanh_cell(0)
+        move_x_product(0)
+        move_x_product(1)
+        hidden_products(1)
+        add_products(0)
+        tanh_cell(1)
         for m in range(M_TILES):
-            if m < STREAMED_TILES:
-                x_product = x_products[m]
-            else:
-                x_product = new_bank()
-                for g in range(X_PASSES):
-                    x_pass(x_product, g, m)
-            h_products = first_h_products if m == 0 else hidden_products(m)
-            finish_tile(m, x_product, h_products)
+            sigmoid(m)
+            if m + 2 < M_TILES:
+                hidden_products(m + 2)
+            if STREAMED_TILES <= m + LATE_AHEAD < M_TILES:
+                late_x_product(m + LATE_AHEAD)
+            if m + 1 < M_TILES:
+                add_products(m + 1)
+            if m + 2 < M_TILES:
+                move_x_product(m + 2)
+                tanh_cell(m + 2)
+            mix_and_store(m)

@@ -114,10 +114,6 @@ def tile_mdlstmcellweights_pb_k_kernel(
                     in_=cell[d][m0 * P : m1 * P, :].rearrange("(m p) n -> p m n", p=P),
                 )
 
-        with nc.allow_non_contiguous_dma(reason="b_o: one 2-byte element for each partition and tile"):
-            nc.scalar.dma_start(out=bias[:], in_=b_o.rearrange("(m p) o -> p (m o)", p=P))
-        nc.scalar.dma_start(out=mix[:], in_=weighted_sum.partition_broadcast(P))
-
         rows_per_pass = SCALE_ROWS // 2 // SCALE_GROUP
         raw_tiles = []
         for g in range(X_PASSES):
@@ -144,6 +140,9 @@ def tile_mdlstmcellweights_pb_k_kernel(
                         )
                 load_words(nc, ho_words, w_ho_words, slice(0, H_PASSES), slice(0, M_TILES * TILE_WORD_BYTES))
         load_cell(0, M_TILES // 2)
+        with nc.allow_non_contiguous_dma(reason="b_o: one 2-byte element for each partition and tile"):
+            nc.sync.dma_start(out=bias[:], in_=b_o.rearrange("(m p) o -> p (m o)", p=P))
+        nc.sync.dma_start(out=mix[:], in_=weighted_sum.partition_broadcast(P))
         load_words(
             nc, late_words, w_io_words, slice(0, X_PASSES),
             slice(STREAMED_TILES * TILE_WORD_BYTES, M_TILES * TILE_WORD_BYTES),

@@ -24,11 +24,12 @@ TILE_WORD_BYTES = P * 2
 SCALE_ROWS = K_PASS // 32
 
 PSUM_BANKS = 8
-STREAMED_TILES = 6
+STREAMED_TILES = 5
 LATE_TILES = M_TILES - STREAMED_TILES
+assert LATE_TILES <= PSUM_BANKS - STREAMED_TILES
 SCALE_GROUP = 4
-H_AFTER = 7
-LATE_AHEAD = 4
+DIFFERENCES_PER_PASS = 2
+CELL_GROUP = 2
 RAW_BUFS = 8
 
 FLOPS = 2 * OUT_C * N * (IN_C + DIRS * OUT_C)
@@ -86,6 +87,7 @@ def tile_mdlstmcellweights_pb_k_kernel(
         x_planes = keep.tile([P, X_PASSES, N], U8, align_bytes=64)
         h_codes = keep.tile([P, DIRS, H_PASSES, N], U32, align_bytes=64)
         h_planes = keep.tile([P, DIRS, H_PASSES, N], U8, align_bytes=64)
+        h_diff = keep.tile([P, M_TILES, N], F32)
         cell_sb = keep.tile([P, M_TILES, DIRS, N], BF16)
         bias = keep.tile([P, M_TILES], BF16)
         mix = keep.tile([P, DIRS], BF16)
@@ -94,10 +96,10 @@ def tile_mdlstmcellweights_pb_k_kernel(
         nc.vector.memset(warm[:], 0.0)
         nc.scalar.activation(out=warm[:], in_=warm[:], func=ACT.Sigmoid)
 
+        nc.vector.memset(ho_planes[:].rearrange("p g n -> p (g n)").bitcast(I32), 0)
         for g0 in range(0, X_PASSES, SCALE_GROUP):
             group = io_planes[:, g0 : g0 + SCALE_GROUP, :]
             nc.vector.memset(group.rearrange("p g n -> p (g n)").bitcast(I32), 0)
-        nc.vector.memset(ho_planes[:].rearrange("p g n -> p (g n)").bitcast(I32), 0)
 
         def load_pass(rows):
             raw = raw_pool.tile([P, PACK, N], BF16, name="raw")
@@ -116,6 +118,12 @@ def tile_mdlstmcellweights_pb_k_kernel(
 
         rows_per_pass = SCALE_ROWS // 2 // SCALE_GROUP
         raw_tiles = []
+        for d in range(DIRS):
+            for c in range(H_PASSES):
+                raw_tiles.append(load_pass(h_prev[d][c * K_PASS : (c + 1) * K_PASS, :]))
+                first_row = (d * H_PASSES + c) * rows_per_pass
+                load_scale_rows(nc, ho_planes, w_ho_scales, slice(0, H_PASSES), range(first_row, first_row + rows_per_pass))
+        load_words(nc, ho_words, w_ho_words, slice(0, H_PASSES), slice(0, M_TILES * TILE_WORD_BYTES))
         for g in range(X_PASSES):
             raw_tiles.append(load_pass(x[g * K_PASS : (g + 1) * K_PASS, :]))
             if g == 0:
@@ -130,16 +138,7 @@ def tile_mdlstmcellweights_pb_k_kernel(
                     nc, io_planes, w_io_scales, slice(next_group, next_group + SCALE_GROUP),
                     range(first_row, first_row + rows_per_pass),
                 )
-            if g == H_AFTER:
-                for d in range(DIRS):
-                    for c in range(H_PASSES):
-                        raw_tiles.append(load_pass(h_prev[d][c * K_PASS : (c + 1) * K_PASS, :]))
-                        first_row = (d * H_PASSES + c) * rows_per_pass
-                        load_scale_rows(
-                            nc, ho_planes, w_ho_scales, slice(0, H_PASSES), range(first_row, first_row + rows_per_pass)
-                        )
-                load_words(nc, ho_words, w_ho_words, slice(0, H_PASSES), slice(0, M_TILES * TILE_WORD_BYTES))
-        load_cell(0, M_TILES // 2)
+        load_cell(0, CELL_GROUP)
         with nc.allow_non_contiguous_dma(reason="b_o: one 2-byte element for each partition and tile"):
             nc.sync.dma_start(out=bias[:], in_=b_o.rearrange("(m p) o -> p (m o)", p=P))
         nc.sync.dma_start(out=mix[:], in_=weighted_sum.partition_broadcast(P))
@@ -147,7 +146,8 @@ def tile_mdlstmcellweights_pb_k_kernel(
             nc, late_words, w_io_words, slice(0, X_PASSES),
             slice(STREAMED_TILES * TILE_WORD_BYTES, M_TILES * TILE_WORD_BYTES),
         )
-        load_cell(M_TILES // 2, M_TILES)
+        for m0 in range(CELL_GROUP, M_TILES, CELL_GROUP):
+            load_cell(m0, m0 + CELL_GROUP)
 
         def weight_pass(acc, words_sb, word_tile, planes, g, m, codes, plane, start, stop):
             nc.tensor.matmul_mx(
@@ -160,8 +160,27 @@ def tile_mdlstmcellweights_pb_k_kernel(
                 stop=stop,
             )
 
-        x_products = {}
         h_products = {}
+        sums = {}
+
+        def h_pass(acc, d, c, m, stop):
+            weight_pass(
+                acc, ho_words, m, ho_planes, c, m, h_codes[:, d, c, :], h_planes[:, d, c, :],
+                start=(c == 0), stop=stop,
+            )
+
+        def hidden_products(m):
+            h_products[m] = []
+            for d in range(DIRS):
+                acc = banks.tile([P, N], F32, name="bank")
+                for c in range(H_PASSES):
+                    h_pass(acc, d, c, m, stop=(c == H_PASSES - 1))
+                h_products[m].append(acc)
+
+        def open_sum(m):
+            sums[m] = banks.tile([P, N], F32, name="bank")
+            for c in range(H_PASSES):
+                h_pass(sums[m], 0, c, m, stop=False)
 
         def x_pass(g, m):
             if m < STREAMED_TILES:
@@ -169,30 +188,18 @@ def tile_mdlstmcellweights_pb_k_kernel(
             else:
                 words_sb, word_tile = late_words, m - STREAMED_TILES
             weight_pass(
-                x_products[m], words_sb, word_tile, io_planes, g, m, x_codes[:, g, :], x_planes[:, g, :],
-                start=(g == 0), stop=(g == X_PASSES - 1),
+                sums[m], words_sb, word_tile, io_planes, g, m, x_codes[:, g, :], x_planes[:, g, :],
+                start=False, stop=(g == X_PASSES - 1),
             )
 
-        def late_x_product(m):
-            x_products[m] = banks.tile([P, N], F32, name="bank")
-            for g in range(X_PASSES):
-                x_pass(g, m)
+        def difference(m):
+            first = work.tile([P, N], F32, name="first")
+            nc.scalar.copy(out=first[:], in_=h_products[m][0][:])
+            nc.vector.tensor_tensor(out=h_diff[:, m, :], in0=h_products[m][1][:], in1=first[:], op=ALU.subtract)
 
-        def hidden_products(m):
-            h_products[m] = []
-            for d in range(DIRS):
-                acc = banks.tile([P, N], F32, name="bank")
-                for c in range(H_PASSES):
-                    weight_pass(
-                        acc, ho_words, m, ho_planes, c, m, h_codes[:, d, c, :], h_planes[:, d, c, :],
-                        start=(c == 0), stop=(c == H_PASSES - 1),
-                    )
-                h_products[m].append(acc)
-
-        targets = [(x_codes[:, g, :], x_planes[:, g, :], g) for g in range(H_AFTER + 1)]
-        targets.extend([(h_codes[:, d, c, :], h_planes[:, d, c, :], None) for d in range(DIRS) for c in range(H_PASSES)])
-        targets.extend([(x_codes[:, g, :], x_planes[:, g, :], g) for g in range(H_AFTER + 1, X_PASSES)])
-        last_h = H_AFTER + DIRS * H_PASSES
+        targets = [(h_codes[:, d, c, :], h_planes[:, d, c, :], None) for d in range(DIRS) for c in range(H_PASSES)]
+        targets.extend([(x_codes[:, g, :], x_planes[:, g, :], g) for g in range(X_PASSES)])
+        last_h = DIRS * H_PASSES - 1
 
         def regroup(raw):
             grouped = grouped_pool.tile([P, N, PACK], BF16, name="grouped", align_bytes=64)
@@ -206,10 +213,8 @@ def tile_mdlstmcellweights_pb_k_kernel(
             )
             return grouped
 
-        for m in range(STREAMED_TILES):
-            x_products[m] = banks.tile([P, N], F32, name="bank")
-
         grouped_tiles = []
+        differences_done = 0
         for i in range(len(raw_tiles) + 1):
             if i < len(raw_tiles):
                 grouped_tiles.append(regroup(raw_tiles[i]))
@@ -220,13 +225,25 @@ def tile_mdlstmcellweights_pb_k_kernel(
                     scales=plane,
                     in_=grouped_tiles[i - 1][:].rearrange("p n t -> p (n t)"),
                 )
+                if i - 1 == last_h:
+                    for m in range(M_TILES):
+                        hidden_products(m)
+                    for m in range(STREAMED_TILES):
+                        open_sum(m)
                 if g is not None:
                     for m in range(STREAMED_TILES):
                         x_pass(g, m)
-                if i - 1 == last_h:
-                    hidden_products(0)
+            if i > last_h:
+                for m in range(differences_done, min(differences_done + DIFFERENCES_PER_PASS, M_TILES)):
+                    difference(m)
+                differences_done = min(differences_done + DIFFERENCES_PER_PASS, M_TILES)
 
-        x_sums, gates, tanhs = {}, {}, {}
+        for m in range(STREAMED_TILES, M_TILES):
+            open_sum(m)
+            for g in range(X_PASSES):
+                x_pass(g, m)
+
+        gates, tanhs = {}, {}
 
         def tanh_cell(m):
             tanhs[m] = work.tile([P, DIRS, N], F32, name="tanh_c")
@@ -236,18 +253,13 @@ def tile_mdlstmcellweights_pb_k_kernel(
                 func=ACT.Tanh,
             )
 
-        def move_x_product(m):
-            x_sums[m] = work.tile([P, N], F32, name="x_sum")
-            nc.scalar.copy(out=x_sums[m][:], in_=x_products[m][:])
-
-        def add_products(m):
+        def second_sum(m):
             gates[m] = work.tile([P, DIRS, N], F32, name="gate")
-            for d in range(DIRS):
-                nc.vector.tensor_tensor(out=gates[m][:, d, :], in0=h_products[m][d][:], in1=x_sums[m][:], op=ALU.add)
+            nc.vector.tensor_tensor(out=gates[m][:, 1, :], in0=sums[m][:], in1=h_diff[:, m, :], op=ALU.add)
 
-        def sigmoid(m):
-            both = gates[m][:].rearrange("p d n -> p (d n)")
-            nc.scalar.activation(out=both, in_=both, func=ACT.Sigmoid, bias=bias[:, m : m + 1])
+        def sigmoids(m):
+            nc.scalar.activation(out=gates[m][:, 1, :], in_=gates[m][:, 1, :], func=ACT.Sigmoid, bias=bias[:, m : m + 1])
+            nc.scalar.activation(out=gates[m][:, 0, :], in_=sums[m][:], func=ACT.Sigmoid, bias=bias[:, m : m + 1])
 
         def mix_and_store(m):
             gate = gates[m]
@@ -261,20 +273,10 @@ def tile_mdlstmcellweights_pb_k_kernel(
             nc.sync.dma_start(out=out[m * P : (m + 1) * P, :], in_=result[:])
 
         tanh_cell(0)
-        move_x_product(0)
-        move_x_product(1)
-        hidden_products(1)
-        add_products(0)
-        tanh_cell(1)
+        second_sum(0)
         for m in range(M_TILES):
-            sigmoid(m)
-            if m + 2 < M_TILES:
-                hidden_products(m + 2)
-            if STREAMED_TILES <= m + LATE_AHEAD < M_TILES:
-                late_x_product(m + LATE_AHEAD)
+            sigmoids(m)
             if m + 1 < M_TILES:
-                add_products(m + 1)
-            if m + 2 < M_TILES:
-                move_x_product(m + 2)
-                tanh_cell(m + 2)
+                second_sum(m + 1)
+                tanh_cell(m + 1)
             mix_and_store(m)

@@ -29,6 +29,7 @@ LATE_TILES = M_TILES - STREAMED_TILES
 assert LATE_TILES <= PSUM_BANKS - STREAMED_TILES
 SCALE_GROUP = 4
 DIFFERENCES_PER_PASS = 2
+LATE_GROUP = X_PASSES // 2
 CELL_GROUP = 2
 RAW_BUFS = 8
 
@@ -142,11 +143,15 @@ def tile_mdlstmcellweights_pb_k_kernel(
         with nc.allow_non_contiguous_dma(reason="b_o: one 2-byte element for each partition and tile"):
             nc.sync.dma_start(out=bias[:], in_=b_o.rearrange("(m p) o -> p (m o)", p=P))
         nc.sync.dma_start(out=mix[:], in_=weighted_sum.partition_broadcast(P))
-        load_words(
-            nc, late_words, w_io_words, slice(0, X_PASSES),
-            slice(STREAMED_TILES * TILE_WORD_BYTES, M_TILES * TILE_WORD_BYTES),
-        )
-        for m0 in range(CELL_GROUP, M_TILES, CELL_GROUP):
+        next_cell = CELL_GROUP
+        for g0 in range(0, X_PASSES, LATE_GROUP):
+            load_words(
+                nc, late_words, w_io_words, slice(g0, g0 + LATE_GROUP),
+                slice(STREAMED_TILES * TILE_WORD_BYTES, M_TILES * TILE_WORD_BYTES),
+            )
+            load_cell(next_cell, next_cell + CELL_GROUP)
+            next_cell += CELL_GROUP
+        for m0 in range(next_cell, M_TILES, CELL_GROUP):
             load_cell(m0, m0 + CELL_GROUP)
 
         def weight_pass(acc, words_sb, word_tile, planes, g, m, codes, plane, start, stop):
@@ -238,10 +243,12 @@ def tile_mdlstmcellweights_pb_k_kernel(
                     difference(m)
                 differences_done = min(differences_done + DIFFERENCES_PER_PASS, M_TILES)
 
-        for m in range(STREAMED_TILES, M_TILES):
-            open_sum(m)
-            for g in range(X_PASSES):
-                x_pass(g, m)
+        for g0 in range(0, X_PASSES, LATE_GROUP):
+            for m in range(STREAMED_TILES, M_TILES):
+                if g0 == 0:
+                    open_sum(m)
+                for g in range(g0, g0 + LATE_GROUP):
+                    x_pass(g, m)
 
         gates, tanhs = {}, {}
 

@@ -21,6 +21,7 @@ H_PASSES = OUT_C // K_PASS
 M_TILES = OUT_C // P
 DIRS = 2
 TILE_WORD_BYTES = P * 2
+QUADRANTS = 4
 SCALE_ROWS = K_PASS // 32
 
 PSUM_BANKS = 8
@@ -37,11 +38,10 @@ FLOPS = 2 * OUT_C * N * (IN_C + DIRS * OUT_C)
 
 
 def load_scale_rows(nc, planes, scales, passes, rows):
-    for q in rows:
-        partition = 32 * (q // 4) + q % 4
+    for r in rows:
         nc.sync.dma_start(
-            out=planes[partition : P : 64, passes, :].bitcast(I32),
-            in_=scales[passes, q : SCALE_ROWS : 8, :].rearrange("g q n -> q g n").bitcast(I32),
+            out=planes[r : P : P // QUADRANTS, passes, :].bitcast(I32),
+            in_=scales[passes, r : SCALE_ROWS : SCALE_ROWS // QUADRANTS, :].rearrange("g q n -> q g n").bitcast(I32),
         )
 
 
@@ -117,7 +117,7 @@ def tile_mdlstmcellweights_pb_k_kernel(
                     in_=cell[d][m0 * P : m1 * P, :].rearrange("(m p) n -> p m n", p=P),
                 )
 
-        rows_per_pass = SCALE_ROWS // 2 // SCALE_GROUP
+        rows_per_pass = SCALE_ROWS // QUADRANTS // SCALE_GROUP
         raw_tiles = []
         for d in range(DIRS):
             for c in range(H_PASSES):
@@ -128,7 +128,7 @@ def tile_mdlstmcellweights_pb_k_kernel(
         for g in range(X_PASSES):
             raw_tiles.append(load_pass(x[g * K_PASS : (g + 1) * K_PASS, :]))
             if g == 0:
-                load_scale_rows(nc, io_planes, w_io_scales, slice(0, SCALE_GROUP), range(SCALE_ROWS // 2))
+                load_scale_rows(nc, io_planes, w_io_scales, slice(0, SCALE_GROUP), range(SCALE_ROWS // QUADRANTS))
                 load_streamed_words(0)
             if g + 1 < X_PASSES:
                 load_streamed_words(g + 1)

@@ -29,6 +29,7 @@ STREAMED_TILES = 5
 LATE_TILES = M_TILES - STREAMED_TILES
 assert LATE_TILES <= PSUM_BANKS - STREAMED_TILES
 SCALE_GROUP = 4
+COPIES_PER_PASS = M_TILES // 2
 DIFFERENCES_PER_PASS = 2
 LATE_GROUP = X_PASSES // 2
 CELL_GROUP = 2
@@ -122,9 +123,9 @@ def tile_mdlstmcellweights_pb_k_kernel(
         for d in range(DIRS):
             for c in range(H_PASSES):
                 raw_tiles.append(load_pass(h_prev[d][c * K_PASS : (c + 1) * K_PASS, :]))
-                first_row = (d * H_PASSES + c) * rows_per_pass
-                load_scale_rows(nc, ho_planes, w_ho_scales, slice(0, H_PASSES), range(first_row, first_row + rows_per_pass))
-        load_words(nc, ho_words, w_ho_words, slice(0, H_PASSES), slice(0, M_TILES * TILE_WORD_BYTES))
+                if d == 0 and c == 0:
+                    load_scale_rows(nc, ho_planes, w_ho_scales, slice(0, H_PASSES), range(SCALE_ROWS // QUADRANTS))
+                    load_words(nc, ho_words, w_ho_words, slice(0, H_PASSES), slice(0, M_TILES * TILE_WORD_BYTES))
         for g in range(X_PASSES):
             raw_tiles.append(load_pass(x[g * K_PASS : (g + 1) * K_PASS, :]))
             if g == 0:
@@ -174,13 +175,10 @@ def tile_mdlstmcellweights_pb_k_kernel(
                 start=(c == 0), stop=stop,
             )
 
-        def hidden_products(m):
-            h_products[m] = []
-            for d in range(DIRS):
-                acc = banks.tile([P, N], F32, name="bank")
-                for c in range(H_PASSES):
-                    h_pass(acc, d, c, m, stop=(c == H_PASSES - 1))
-                h_products[m].append(acc)
+        def product_pass(d, c, m):
+            if c == 0:
+                h_products[d, m] = banks.tile([P, N], F32, name="bank")
+            h_pass(h_products[d, m], d, c, m, stop=(c == H_PASSES - 1))
 
         def open_sum(m):
             sums[m] = banks.tile([P, N], F32, name="bank")
@@ -197,10 +195,11 @@ def tile_mdlstmcellweights_pb_k_kernel(
                 start=False, stop=(g == X_PASSES - 1),
             )
 
+        def copy_product(m):
+            nc.scalar.copy(out=h_diff[:, m, :], in_=h_products[0, m][:])
+
         def difference(m):
-            first = work.tile([P, N], F32, name="first")
-            nc.scalar.copy(out=first[:], in_=h_products[m][0][:])
-            nc.vector.tensor_tensor(out=h_diff[:, m, :], in0=h_products[m][1][:], in1=first[:], op=ALU.subtract)
+            nc.vector.tensor_tensor(out=h_diff[:, m, :], in0=h_products[1, m][:], in1=h_diff[:, m, :], op=ALU.subtract)
 
         targets = [(h_codes[:, d, c, :], h_planes[:, d, c, :], None) for d in range(DIRS) for c in range(H_PASSES)]
         targets.extend([(x_codes[:, g, :], x_planes[:, g, :], g) for g in range(X_PASSES)])
@@ -219,6 +218,7 @@ def tile_mdlstmcellweights_pb_k_kernel(
             return grouped
 
         grouped_tiles = []
+        copies_done = 0
         differences_done = 0
         for i in range(len(raw_tiles) + 1):
             if i < len(raw_tiles):
@@ -230,14 +230,22 @@ def tile_mdlstmcellweights_pb_k_kernel(
                     scales=plane,
                     in_=grouped_tiles[i - 1][:].rearrange("p n t -> p (n t)"),
                 )
+                if i - 1 < H_PASSES:
+                    for m in range(M_TILES):
+                        product_pass(0, i - 1, m)
                 if i - 1 == last_h:
                     for m in range(M_TILES):
-                        hidden_products(m)
+                        for c in range(H_PASSES):
+                            product_pass(1, c, m)
                     for m in range(STREAMED_TILES):
                         open_sum(m)
                 if g is not None:
                     for m in range(STREAMED_TILES):
                         x_pass(g, m)
+            if i >= last_h:
+                for m in range(copies_done, min(copies_done + COPIES_PER_PASS, M_TILES)):
+                    copy_product(m)
+                copies_done = min(copies_done + COPIES_PER_PASS, M_TILES)
             if i > last_h:
                 for m in range(differences_done, min(differences_done + DIFFERENCES_PER_PASS, M_TILES)):
                     difference(m)

@@ -29,8 +29,8 @@ STREAMED_TILES = 5
 LATE_TILES = M_TILES - STREAMED_TILES
 assert LATE_TILES <= PSUM_BANKS - STREAMED_TILES
 SCALE_GROUP = 4
-COPIES_PER_PASS = M_TILES // 2
-DIFFERENCES_PER_PASS = 2
+DIFFERENCES_PER_PASS = 3
+VECTOR_ZEROED_GROUPS = X_PASSES // SCALE_GROUP // 2
 LATE_GROUP = X_PASSES // 2
 CELL_GROUP = 2
 RAW_BUFS = 8
@@ -99,9 +99,10 @@ def tile_mdlstmcellweights_pb_k_kernel(
         nc.scalar.activation(out=warm[:], in_=warm[:], func=ACT.Sigmoid)
 
         nc.vector.memset(ho_planes[:].rearrange("p g n -> p (g n)").bitcast(I32), 0)
-        for g0 in range(0, X_PASSES, SCALE_GROUP):
-            group = io_planes[:, g0 : g0 + SCALE_GROUP, :]
-            nc.vector.memset(group.rearrange("p g n -> p (g n)").bitcast(I32), 0)
+        for i in range(X_PASSES // SCALE_GROUP):
+            group = io_planes[:, i * SCALE_GROUP : (i + 1) * SCALE_GROUP, :]
+            engine = nc.vector if i < VECTOR_ZEROED_GROUPS else nc.gpsimd
+            engine.memset(group.rearrange("p g n -> p (g n)").bitcast(I32), 0)
 
         def load_pass(rows):
             raw = raw_pool.tile([P, PACK, N], BF16, name="raw")
@@ -195,15 +196,11 @@ def tile_mdlstmcellweights_pb_k_kernel(
                 start=False, stop=(g == X_PASSES - 1),
             )
 
-        def copy_product(m):
-            nc.scalar.copy(out=h_diff[:, m, :], in_=h_products[0, m][:])
-
         def difference(m):
             nc.vector.tensor_tensor(out=h_diff[:, m, :], in0=h_products[1, m][:], in1=h_diff[:, m, :], op=ALU.subtract)
 
-        targets = [(h_codes[:, d, c, :], h_planes[:, d, c, :], None) for d in range(DIRS) for c in range(H_PASSES)]
-        targets.extend([(x_codes[:, g, :], x_planes[:, g, :], g) for g in range(X_PASSES)])
-        last_h = DIRS * H_PASSES - 1
+        targets = [(h_codes[:, d, c, :], h_planes[:, d, c, :]) for d in range(DIRS) for c in range(H_PASSES)]
+        targets.extend([(x_codes[:, g, :], x_planes[:, g, :]) for g in range(X_PASSES)])
 
         def regroup(raw):
             grouped = grouped_pool.tile([P, N, PACK], BF16, name="grouped", align_bytes=64)
@@ -217,39 +214,35 @@ def tile_mdlstmcellweights_pb_k_kernel(
             )
             return grouped
 
+        def quantise(i, grouped):
+            codes, plane = targets[i]
+            nc.vector.quantize_mx(out=codes.bitcast(FP8X4), scales=plane, in_=grouped[:].rearrange("p n t -> p (n t)"))
+
+        for i in range(DIRS * H_PASSES):
+            quantise(i, regroup(raw_tiles[i]))
+            if i < H_PASSES:
+                for m in range(M_TILES):
+                    product_pass(0, i, m)
+        for m in range(M_TILES // 2):
+            nc.scalar.copy(out=h_diff[:, m, :], in_=h_products[0, m][:])
+        for m in range(M_TILES // 2, M_TILES):
+            nc.vector.tensor_copy(out=h_diff[:, m, :], in_=h_products[0, m][:])
+        for m in range(M_TILES):
+            for c in range(H_PASSES):
+                product_pass(1, c, m)
+        for m in range(STREAMED_TILES):
+            open_sum(m)
+
         grouped_tiles = []
-        copies_done = 0
-        differences_done = 0
-        for i in range(len(raw_tiles) + 1):
-            if i < len(raw_tiles):
-                grouped_tiles.append(regroup(raw_tiles[i]))
-            if i > 0:
-                codes, plane, g = targets[i - 1]
-                nc.vector.quantize_mx(
-                    out=codes.bitcast(FP8X4),
-                    scales=plane,
-                    in_=grouped_tiles[i - 1][:].rearrange("p n t -> p (n t)"),
-                )
-                if i - 1 < H_PASSES:
-                    for m in range(M_TILES):
-                        product_pass(0, i - 1, m)
-                if i - 1 == last_h:
-                    for m in range(M_TILES):
-                        for c in range(H_PASSES):
-                            product_pass(1, c, m)
-                    for m in range(STREAMED_TILES):
-                        open_sum(m)
-                if g is not None:
-                    for m in range(STREAMED_TILES):
-                        x_pass(g, m)
-            if i >= last_h:
-                for m in range(copies_done, min(copies_done + COPIES_PER_PASS, M_TILES)):
-                    copy_product(m)
-                copies_done = min(copies_done + COPIES_PER_PASS, M_TILES)
-            if i > last_h:
-                for m in range(differences_done, min(differences_done + DIFFERENCES_PER_PASS, M_TILES)):
-                    difference(m)
-                differences_done = min(differences_done + DIFFERENCES_PER_PASS, M_TILES)
+        for g in range(X_PASSES + 1):
+            if g < X_PASSES:
+                grouped_tiles.append(regroup(raw_tiles[DIRS * H_PASSES + g]))
+            if g > 0:
+                quantise(DIRS * H_PASSES + g - 1, grouped_tiles[g - 1])
+                for m in range(STREAMED_TILES):
+                    x_pass(g - 1, m)
+            for m in range(g * DIFFERENCES_PER_PASS, min((g + 1) * DIFFERENCES_PER_PASS, M_TILES)):
+                difference(m)
 
         for g0 in range(0, X_PASSES, LATE_GROUP):
             for m in range(STREAMED_TILES, M_TILES):

@@ -29,8 +29,11 @@ STREAMED_TILES = 5
 LATE_TILES = M_TILES - STREAMED_TILES
 assert LATE_TILES <= PSUM_BANKS - STREAMED_TILES
 SCALE_GROUP = 4
-DIFFERENCES_PER_PASS = 3
-VECTOR_ZEROED_GROUPS = X_PASSES // SCALE_GROUP // 2
+DIFFERENCES_PER_PASS = 4
+X_VECTOR_COLUMNS = N // 2
+H_VECTOR_COLUMNS = 5 * N // 8
+LAST_PASSES = 2
+LAST_TILE_PIECE = N // 2
 LATE_GROUP = X_PASSES // 2
 CELL_GROUP = 2
 RAW_BUFS = 8
@@ -99,10 +102,9 @@ def tile_mdlstmcellweights_pb_k_kernel(
         nc.scalar.activation(out=warm[:], in_=warm[:], func=ACT.Sigmoid)
 
         nc.vector.memset(ho_planes[:].rearrange("p g n -> p (g n)").bitcast(I32), 0)
-        for i in range(X_PASSES // SCALE_GROUP):
-            group = io_planes[:, i * SCALE_GROUP : (i + 1) * SCALE_GROUP, :]
-            engine = nc.vector if i < VECTOR_ZEROED_GROUPS else nc.gpsimd
-            engine.memset(group.rearrange("p g n -> p (g n)").bitcast(I32), 0)
+        for g0 in range(0, X_PASSES, SCALE_GROUP):
+            group = io_planes[:, g0 : g0 + SCALE_GROUP, :]
+            nc.vector.memset(group.rearrange("p g n -> p (g n)").bitcast(I32), 0)
 
         def load_pass(rows):
             raw = raw_pool.tile([P, PACK, N], BF16, name="raw")
@@ -126,7 +128,8 @@ def tile_mdlstmcellweights_pb_k_kernel(
                 raw_tiles.append(load_pass(h_prev[d][c * K_PASS : (c + 1) * K_PASS, :]))
                 if d == 0 and c == 0:
                     load_scale_rows(nc, ho_planes, w_ho_scales, slice(0, H_PASSES), range(SCALE_ROWS // QUADRANTS))
-                    load_words(nc, ho_words, w_ho_words, slice(0, H_PASSES), slice(0, M_TILES * TILE_WORD_BYTES))
+                if d == 0:
+                    load_words(nc, ho_words, w_ho_words, slice(c, c + 1), slice(0, M_TILES * TILE_WORD_BYTES))
         for g in range(X_PASSES):
             raw_tiles.append(load_pass(x[g * K_PASS : (g + 1) * K_PASS, :]))
             if g == 0:
@@ -202,15 +205,15 @@ def tile_mdlstmcellweights_pb_k_kernel(
         targets = [(h_codes[:, d, c, :], h_planes[:, d, c, :]) for d in range(DIRS) for c in range(H_PASSES)]
         targets.extend([(x_codes[:, g, :], x_planes[:, g, :]) for g in range(X_PASSES)])
 
-        def regroup(raw):
+        def regroup(raw, split):
             grouped = grouped_pool.tile([P, N, PACK], BF16, name="grouped", align_bytes=64)
             nc.vector.tensor_copy(
-                out=grouped[:, : N // 2, :].rearrange("p (c i) t -> p c t i", i=4),
-                in_=raw[:, :, : N // 2].rearrange("p t (c i) -> p c t i", i=4),
+                out=grouped[:, :split, :].rearrange("p (c i) t -> p c t i", i=4),
+                in_=raw[:, :, :split].rearrange("p t (c i) -> p c t i", i=4),
             )
             nc.scalar.copy(
-                out=grouped[:, N // 2 :, :].rearrange("p (c i) t -> p c t i", i=4),
-                in_=raw[:, :, N // 2 :].rearrange("p t (c i) -> p c t i", i=4),
+                out=grouped[:, split:, :].rearrange("p (c i) t -> p c t i", i=4),
+                in_=raw[:, :, split:].rearrange("p t (c i) -> p c t i", i=4),
             )
             return grouped
 
@@ -219,7 +222,7 @@ def tile_mdlstmcellweights_pb_k_kernel(
             nc.vector.quantize_mx(out=codes.bitcast(FP8X4), scales=plane, in_=grouped[:].rearrange("p n t -> p (n t)"))
 
         for i in range(DIRS * H_PASSES):
-            quantise(i, regroup(raw_tiles[i]))
+            quantise(i, regroup(raw_tiles[i], H_VECTOR_COLUMNS))
             if i < H_PASSES:
                 for m in range(M_TILES):
                     product_pass(0, i, m)
@@ -236,20 +239,23 @@ def tile_mdlstmcellweights_pb_k_kernel(
         grouped_tiles = []
         for g in range(X_PASSES + 1):
             if g < X_PASSES:
-                grouped_tiles.append(regroup(raw_tiles[DIRS * H_PASSES + g]))
+                grouped_tiles.append(regroup(raw_tiles[DIRS * H_PASSES + g], X_VECTOR_COLUMNS))
             if g > 0:
                 quantise(DIRS * H_PASSES + g - 1, grouped_tiles[g - 1])
-                for m in range(STREAMED_TILES):
-                    x_pass(g - 1, m)
+                if g - 1 < X_PASSES - LAST_PASSES:
+                    for m in range(STREAMED_TILES):
+                        x_pass(g - 1, m)
             for m in range(g * DIFFERENCES_PER_PASS, min((g + 1) * DIFFERENCES_PER_PASS, M_TILES)):
                 difference(m)
 
-        for g0 in range(0, X_PASSES, LATE_GROUP):
-            for m in range(STREAMED_TILES, M_TILES):
-                if g0 == 0:
-                    open_sum(m)
-                for g in range(g0, g0 + LATE_GROUP):
-                    x_pass(g, m)
+        for m in range(STREAMED_TILES):
+            for g in range(X_PASSES - LAST_PASSES, X_PASSES):
+                x_pass(g, m)
+
+        for m in range(STREAMED_TILES, M_TILES):
+            open_sum(m)
+            for g in range(X_PASSES):
+                x_pass(g, m)
 
         gates, tanhs = {}, {}
 
@@ -261,30 +267,46 @@ def tile_mdlstmcellweights_pb_k_kernel(
                 func=ACT.Tanh,
             )
 
-        def second_sum(m):
-            gates[m] = work.tile([P, DIRS, N], F32, name="gate")
-            nc.vector.tensor_tensor(out=gates[m][:, 1, :], in0=sums[m][:], in1=h_diff[:, m, :], op=ALU.add)
+        def second_sum(m, cols=slice(0, N)):
+            if m not in gates:
+                gates[m] = work.tile([P, DIRS, N], F32, name="gate")
+            nc.vector.tensor_tensor(out=gates[m][:, 1, cols], in0=sums[m][:, cols], in1=h_diff[:, m, cols], op=ALU.add)
 
-        def sigmoids(m):
-            nc.scalar.activation(out=gates[m][:, 1, :], in_=gates[m][:, 1, :], func=ACT.Sigmoid, bias=bias[:, m : m + 1])
-            nc.scalar.activation(out=gates[m][:, 0, :], in_=sums[m][:], func=ACT.Sigmoid, bias=bias[:, m : m + 1])
+        def sigmoids(m, cols=slice(0, N)):
+            nc.scalar.activation(out=gates[m][:, 1, cols], in_=gates[m][:, 1, cols], func=ACT.Sigmoid, bias=bias[:, m : m + 1])
+            nc.scalar.activation(out=gates[m][:, 0, cols], in_=sums[m][:, cols], func=ACT.Sigmoid, bias=bias[:, m : m + 1])
 
-        def mix_and_store(m):
-            gate = gates[m]
-            for d in range(DIRS):
-                nc.vector.scalar_tensor_tensor(
-                    out=gate[:, d, :], in0=gate[:, d, :], scalar=mix[:, d : d + 1], in1=tanhs[m][:, d, :],
-                    op0=ALU.mult, op1=ALU.mult,
-                )
-            result = work.tile([P, N], F32, name="result")
-            nc.vector.tensor_tensor(out=result[:], in0=gate[:, 0, :], in1=gate[:, 1, :], op=ALU.add)
-            nc.sync.dma_start(out=out[m * P : (m + 1) * P, :], in_=result[:])
+        def gated(m, d, cols=slice(0, N)):
+            nc.vector.scalar_tensor_tensor(
+                out=gates[m][:, d, cols], in0=gates[m][:, d, cols], scalar=mix[:, d : d + 1], in1=tanhs[m][:, d, cols],
+                op0=ALU.mult, op1=ALU.mult,
+            )
 
+        def add_and_store(m, cols=slice(0, N)):
+            result = work.tile([P, cols.stop - cols.start], F32, name="result")
+            nc.vector.tensor_tensor(out=result[:], in0=gates[m][:, 0, cols], in1=gates[m][:, 1, cols], op=ALU.add)
+            nc.sync.dma_start(out=out[m * P : (m + 1) * P, cols], in_=result[:])
+
+        last = M_TILES - 1
         tanh_cell(0)
         second_sum(0)
-        for m in range(M_TILES):
+        for m in range(last):
             sigmoids(m)
-            if m + 1 < M_TILES:
+            tanh_cell(m + 1)
+            gated(m, 1)
+            gated(m, 0)
+            if m + 1 < last:
                 second_sum(m + 1)
-                tanh_cell(m + 1)
-            mix_and_store(m)
+                add_and_store(m)
+        add_and_store(last - 1)
+        pieces = [slice(c, c + LAST_TILE_PIECE) for c in range(0, N, LAST_TILE_PIECE)]
+        for cols in pieces:
+            second_sum(last, cols)
+        for cols in pieces:
+            sigmoids(last, cols)
+        gated(last, 1, pieces[0])
+        for cols, next_cols in zip(pieces, pieces[1:] + [None]):
+            gated(last, 0, cols)
+            if next_cols is not None:
+                gated(last, 1, next_cols)
+            add_and_store(last, cols)

@@ -23,16 +23,19 @@ DIRS = 2
 TILE_WORD_BYTES = P * 2
 QUADRANTS = 4
 SCALE_ROWS = K_PASS // 32
+ROWS_PER_QUADRANT = SCALE_ROWS // QUADRANTS
 
 PSUM_BANKS = 8
-STREAMED_TILES = 5
+STREAMED_TILES = 6
+STREAMED = slice(0, STREAMED_TILES * P)
 LATE_TILES = M_TILES - STREAMED_TILES
+LATE = slice(STREAMED_TILES * P, OUT_C)
 assert LATE_TILES <= PSUM_BANKS - STREAMED_TILES
+WORD_GROUP = 2
 SCALE_GROUP = 4
-DIFFERENCES_PER_PASS = 4
-X_VECTOR_COLUMNS = N // 2
+X_VECTOR_COLUMNS = 9 * N // 16
 H_VECTOR_COLUMNS = 5 * N // 8
-LAST_PASSES = 2
+LAST_PASSES = 4
 LAST_TILE_PIECE = N // 2
 LATE_GROUP = X_PASSES // 2
 CELL_GROUP = 2
@@ -41,11 +44,11 @@ RAW_BUFS = 8
 FLOPS = 2 * OUT_C * N * (IN_C + DIRS * OUT_C)
 
 
-def load_scale_rows(nc, planes, scales, passes, rows):
+def load_scale_rows(nc, planes, scales, passes, rows, channels):
     for r in rows:
         nc.sync.dma_start(
             out=planes[r : P : P // QUADRANTS, passes, :].bitcast(I32),
-            in_=scales[passes, r : SCALE_ROWS : SCALE_ROWS // QUADRANTS, :].rearrange("g q n -> q g n").bitcast(I32),
+            in_=scales[passes, r : SCALE_ROWS : ROWS_PER_QUADRANT, channels].rearrange("g q n -> q g n").bitcast(I32),
         )
 
 
@@ -85,7 +88,8 @@ def tile_mdlstmcellweights_pb_k_kernel(
 
         streamed_words = keep.tile([P, X_PASSES, STREAMED_TILES * TILE_WORD_BYTES], U8, align_bytes=64)
         late_words = keep.tile([P, X_PASSES, LATE_TILES * TILE_WORD_BYTES], U8, align_bytes=64)
-        io_planes = keep.tile([P, X_PASSES, OUT_C], U8, align_bytes=64)
+        streamed_planes = keep.tile([P, X_PASSES, STREAMED_TILES * P], U8, align_bytes=64)
+        late_planes = keep.tile([P, X_PASSES, LATE_TILES * P], U8, align_bytes=64)
         ho_words = keep.tile([P, H_PASSES, M_TILES * TILE_WORD_BYTES], U8, align_bytes=64)
         ho_planes = keep.tile([P, H_PASSES, OUT_C], U8, align_bytes=64)
         x_codes = keep.tile([P, X_PASSES, N], U32, align_bytes=64)
@@ -103,8 +107,9 @@ def tile_mdlstmcellweights_pb_k_kernel(
 
         nc.vector.memset(ho_planes[:].rearrange("p g n -> p (g n)").bitcast(I32), 0)
         for g0 in range(0, X_PASSES, SCALE_GROUP):
-            group = io_planes[:, g0 : g0 + SCALE_GROUP, :]
+            group = streamed_planes[:, g0 : g0 + SCALE_GROUP, :]
             nc.vector.memset(group.rearrange("p g n -> p (g n)").bitcast(I32), 0)
+        nc.vector.memset(late_planes[:].rearrange("p g n -> p (g n)").bitcast(I32), 0)
 
         def load_pass(rows):
             raw = raw_pool.tile([P, PACK, N], BF16, name="raw")
@@ -112,7 +117,11 @@ def tile_mdlstmcellweights_pb_k_kernel(
             return raw
 
         def load_streamed_words(g):
-            load_words(nc, streamed_words, w_io_words, slice(g, g + 1), slice(0, STREAMED_TILES * TILE_WORD_BYTES))
+            passes = slice(g, g + WORD_GROUP)
+            load_words(nc, streamed_words, w_io_words, passes, slice(0, STREAMED_TILES * TILE_WORD_BYTES))
+
+        def load_streamed_scales(g, rows):
+            load_scale_rows(nc, streamed_planes, w_io_scales, slice(g, g + SCALE_GROUP), rows, STREAMED)
 
         def load_cell(m0, m1):
             for d in range(DIRS):
@@ -121,29 +130,27 @@ def tile_mdlstmcellweights_pb_k_kernel(
                     in_=cell[d][m0 * P : m1 * P, :].rearrange("(m p) n -> p m n", p=P),
                 )
 
-        rows_per_pass = SCALE_ROWS // QUADRANTS // SCALE_GROUP
+        assert SCALE_GROUP == ROWS_PER_QUADRANT
         raw_tiles = []
         for d in range(DIRS):
             for c in range(H_PASSES):
                 raw_tiles.append(load_pass(h_prev[d][c * K_PASS : (c + 1) * K_PASS, :]))
                 if d == 0 and c == 0:
-                    load_scale_rows(nc, ho_planes, w_ho_scales, slice(0, H_PASSES), range(SCALE_ROWS // QUADRANTS))
+                    all_rows = range(ROWS_PER_QUADRANT)
+                    load_scale_rows(nc, ho_planes, w_ho_scales, slice(0, H_PASSES), all_rows, slice(0, OUT_C))
                 if d == 0:
                     load_words(nc, ho_words, w_ho_words, slice(c, c + 1), slice(0, M_TILES * TILE_WORD_BYTES))
         for g in range(X_PASSES):
             raw_tiles.append(load_pass(x[g * K_PASS : (g + 1) * K_PASS, :]))
             if g == 0:
-                load_scale_rows(nc, io_planes, w_io_scales, slice(0, SCALE_GROUP), range(SCALE_ROWS // QUADRANTS))
+                load_streamed_scales(0, range(ROWS_PER_QUADRANT))
                 load_streamed_words(0)
-            if g + 1 < X_PASSES:
+            if (g + 1) % WORD_GROUP == 0 and g + 1 < X_PASSES:
                 load_streamed_words(g + 1)
             next_group = (g // SCALE_GROUP + 1) * SCALE_GROUP
             if next_group < X_PASSES:
-                first_row = (g % SCALE_GROUP) * rows_per_pass
-                load_scale_rows(
-                    nc, io_planes, w_io_scales, slice(next_group, next_group + SCALE_GROUP),
-                    range(first_row, first_row + rows_per_pass),
-                )
+                load_streamed_scales(next_group, [g % SCALE_GROUP])
+        load_scale_rows(nc, late_planes, w_io_scales, slice(0, X_PASSES), range(ROWS_PER_QUADRANT), LATE)
         load_cell(0, CELL_GROUP)
         with nc.allow_non_contiguous_dma(reason="b_o: one 2-byte element for each partition and tile"):
             nc.sync.dma_start(out=bias[:], in_=b_o.rearrange("(m p) o -> p (m o)", p=P))
@@ -159,62 +166,61 @@ def tile_mdlstmcellweights_pb_k_kernel(
         for m0 in range(next_cell, M_TILES, CELL_GROUP):
             load_cell(m0, m0 + CELL_GROUP)
 
-        def weight_pass(acc, words_sb, word_tile, planes, g, m, codes, plane, start, stop):
+        def weight_pass(acc, words_sb, planes, g, w, codes, plane, start, stop):
             nc.tensor.matmul_mx(
                 out=acc[:],
-                lhsT=words_sb[:, g, word_tile * TILE_WORD_BYTES : (word_tile + 1) * TILE_WORD_BYTES].bitcast(FP4X4),
-                lhsT_scale=planes[:, g, m * P : (m + 1) * P],
+                lhsT=words_sb[:, g, w * TILE_WORD_BYTES : (w + 1) * TILE_WORD_BYTES].bitcast(FP4X4),
+                lhsT_scale=planes[:, g, w * P : (w + 1) * P],
                 rhs=codes.bitcast(FP8X4),
                 rhs_scale=plane,
                 start=start,
                 stop=stop,
             )
 
-        h_products = {}
+        differences = {}
         sums = {}
 
-        def h_pass(acc, d, c, m, stop):
+        def h_pass(acc, d, c, m, start, stop):
             weight_pass(
-                acc, ho_words, m, ho_planes, c, m, h_codes[:, d, c, :], h_planes[:, d, c, :],
-                start=(c == 0), stop=stop,
+                acc, ho_words, ho_planes, c, m, h_codes[:, d, c, :], h_planes[:, d, c, :],
+                start=start, stop=stop,
             )
 
-        def product_pass(d, c, m):
-            if c == 0:
-                h_products[d, m] = banks.tile([P, N], F32, name="bank")
-            h_pass(h_products[d, m], d, c, m, stop=(c == H_PASSES - 1))
+        def difference_pass(i, m):
+            if i == 0:
+                differences[m] = banks.tile([P, N], F32, name="bank")
+            h_pass(differences[m], i // H_PASSES, i % H_PASSES, m, start=(i == 0), stop=(i == DIRS * H_PASSES - 1))
 
         def open_sum(m):
             sums[m] = banks.tile([P, N], F32, name="bank")
             for c in range(H_PASSES):
-                h_pass(sums[m], 0, c, m, stop=False)
+                h_pass(sums[m], 1, c, m, start=(c == 0), stop=False)
 
         def x_pass(g, m):
             if m < STREAMED_TILES:
-                words_sb, word_tile = streamed_words, m
+                words_sb, planes, w = streamed_words, streamed_planes, m
             else:
-                words_sb, word_tile = late_words, m - STREAMED_TILES
+                words_sb, planes, w = late_words, late_planes, m - STREAMED_TILES
             weight_pass(
-                sums[m], words_sb, word_tile, io_planes, g, m, x_codes[:, g, :], x_planes[:, g, :],
+                sums[m], words_sb, planes, g, w, x_codes[:, g, :], x_planes[:, g, :],
                 start=False, stop=(g == X_PASSES - 1),
             )
-
-        def difference(m):
-            nc.vector.tensor_tensor(out=h_diff[:, m, :], in0=h_products[1, m][:], in1=h_diff[:, m, :], op=ALU.subtract)
 
         targets = [(h_codes[:, d, c, :], h_planes[:, d, c, :]) for d in range(DIRS) for c in range(H_PASSES)]
         targets.extend([(x_codes[:, g, :], x_planes[:, g, :]) for g in range(X_PASSES)])
 
-        def regroup(raw, split):
+        def regroup(raw, split, negate=False):
             grouped = grouped_pool.tile([P, N, PACK], BF16, name="grouped", align_bytes=64)
-            nc.vector.tensor_copy(
-                out=grouped[:, :split, :].rearrange("p (c i) t -> p c t i", i=4),
-                in_=raw[:, :, :split].rearrange("p t (c i) -> p c t i", i=4),
-            )
-            nc.scalar.copy(
-                out=grouped[:, split:, :].rearrange("p (c i) t -> p c t i", i=4),
-                in_=raw[:, :, split:].rearrange("p t (c i) -> p c t i", i=4),
-            )
+            vector_out = grouped[:, :split, :].rearrange("p (c i) t -> p c t i", i=4)
+            vector_in = raw[:, :, :split].rearrange("p t (c i) -> p c t i", i=4)
+            scalar_out = grouped[:, split:, :].rearrange("p (c i) t -> p c t i", i=4)
+            scalar_in = raw[:, :, split:].rearrange("p t (c i) -> p c t i", i=4)
+            if negate:
+                nc.vector.tensor_scalar(out=vector_out, in0=vector_in, scalar1=-1.0, scalar2=None, op0=ALU.mult)
+                nc.scalar.activation(out=scalar_out, in_=scalar_in, func=ACT.Copy, scale=-1.0)
+            else:
+                nc.vector.tensor_copy(out=vector_out, in_=vector_in)
+                nc.scalar.copy(out=scalar_out, in_=scalar_in)
             return grouped
 
         def quantise(i, grouped):
@@ -222,17 +228,14 @@ def tile_mdlstmcellweights_pb_k_kernel(
             nc.vector.quantize_mx(out=codes.bitcast(FP8X4), scales=plane, in_=grouped[:].rearrange("p n t -> p (n t)"))
 
         for i in range(DIRS * H_PASSES):
-            quantise(i, regroup(raw_tiles[i], H_VECTOR_COLUMNS))
-            if i < H_PASSES:
-                for m in range(M_TILES):
-                    product_pass(0, i, m)
-        for m in range(M_TILES // 2):
-            nc.scalar.copy(out=h_diff[:, m, :], in_=h_products[0, m][:])
-        for m in range(M_TILES // 2, M_TILES):
-            nc.vector.tensor_copy(out=h_diff[:, m, :], in_=h_products[0, m][:])
+            quantise(i, regroup(raw_tiles[i], H_VECTOR_COLUMNS, negate=(i < H_PASSES)))
+            for m in range(M_TILES):
+                difference_pass(i, m)
         for m in range(M_TILES):
-            for c in range(H_PASSES):
-                product_pass(1, c, m)
+            if m % 2 == 0:
+                nc.vector.tensor_copy(out=h_diff[:, m, :], in_=differences[m][:])
+            else:
+                nc.scalar.copy(out=h_diff[:, m, :], in_=differences[m][:])
         for m in range(STREAMED_TILES):
             open_sum(m)
 
@@ -245,8 +248,6 @@ def tile_mdlstmcellweights_pb_k_kernel(
                 if g - 1 < X_PASSES - LAST_PASSES:
                     for m in range(STREAMED_TILES):
                         x_pass(g - 1, m)
-            for m in range(g * DIFFERENCES_PER_PASS, min((g + 1) * DIFFERENCES_PER_PASS, M_TILES)):
-                difference(m)
 
         for m in range(STREAMED_TILES):
             for g in range(X_PASSES - LAST_PASSES, X_PASSES):
@@ -270,11 +271,11 @@ def tile_mdlstmcellweights_pb_k_kernel(
         def second_sum(m, cols=slice(0, N)):
             if m not in gates:
                 gates[m] = work.tile([P, DIRS, N], F32, name="gate")
-            nc.vector.tensor_tensor(out=gates[m][:, 1, cols], in0=sums[m][:, cols], in1=h_diff[:, m, cols], op=ALU.add)
+            nc.vector.tensor_tensor(out=gates[m][:, 0, cols], in0=sums[m][:, cols], in1=h_diff[:, m, cols], op=ALU.subtract)
 
         def sigmoids(m, cols=slice(0, N)):
-            nc.scalar.activation(out=gates[m][:, 1, cols], in_=gates[m][:, 1, cols], func=ACT.Sigmoid, bias=bias[:, m : m + 1])
-            nc.scalar.activation(out=gates[m][:, 0, cols], in_=sums[m][:, cols], func=ACT.Sigmoid, bias=bias[:, m : m + 1])
+            nc.scalar.activation(out=gates[m][:, 0, cols], in_=gates[m][:, 0, cols], func=ACT.Sigmoid, bias=bias[:, m : m + 1])
+            nc.scalar.activation(out=gates[m][:, 1, cols], in_=sums[m][:, cols], func=ACT.Sigmoid, bias=bias[:, m : m + 1])
 
         def gated(m, d, cols=slice(0, N)):
             nc.vector.scalar_tensor_tensor(
@@ -292,21 +293,18 @@ def tile_mdlstmcellweights_pb_k_kernel(
         second_sum(0)
         for m in range(last):
             sigmoids(m)
-            tanh_cell(m + 1)
-            gated(m, 1)
-            gated(m, 0)
             if m + 1 < last:
                 second_sum(m + 1)
-                add_and_store(m)
-        add_and_store(last - 1)
+            tanh_cell(m + 1)
+            gated(m, 0)
+            gated(m, 1)
+            add_and_store(m)
         pieces = [slice(c, c + LAST_TILE_PIECE) for c in range(0, N, LAST_TILE_PIECE)]
         for cols in pieces:
             second_sum(last, cols)
         for cols in pieces:
             sigmoids(last, cols)
-        gated(last, 1, pieces[0])
-        for cols, next_cols in zip(pieces, pieces[1:] + [None]):
+        for cols in pieces:
             gated(last, 0, cols)
-            if next_cols is not None:
-                gated(last, 1, next_cols)
+            gated(last, 1, cols)
             add_and_store(last, cols)

@@ -83,7 +83,7 @@ def tile_mdlstmcellweights_pb_k_kernel(
         keep = stack.enter_context(tc.tile_pool(name="keep", bufs=1))
         raw_pool = stack.enter_context(tc.tile_pool(name="raw", bufs=RAW_BUFS))
         grouped_pool = stack.enter_context(tc.tile_pool(name="grouped", bufs=3))
-        work = stack.enter_context(tc.tile_pool(name="work", bufs=3))
+        work = stack.enter_context(tc.tile_pool(name="work", bufs=4))
         banks = stack.enter_context(tc.psum_pool(name="banks", bufs=PSUM_BANKS))
 
         streamed_words = keep.tile([P, X_PASSES, STREAMED_TILES * TILE_WORD_BYTES], U8, align_bytes=64)
@@ -297,14 +297,20 @@ def tile_mdlstmcellweights_pb_k_kernel(
                 second_sum(m + 1)
             tanh_cell(m + 1)
             gated(m, 0)
+            if m > 0:
+                add_and_store(m - 1)
             gated(m, 1)
-            add_and_store(m)
         pieces = [slice(c, c + LAST_TILE_PIECE) for c in range(0, N, LAST_TILE_PIECE)]
-        for cols in pieces:
+        second_sum(last, pieces[0])
+        add_and_store(last - 1)
+        for cols in pieces[1:]:
             second_sum(last, cols)
         for cols in pieces:
             sigmoids(last, cols)
-        for cols in pieces:
-            gated(last, 0, cols)
-            gated(last, 1, cols)
+        gated(last, 0, pieces[0])
+        gated(last, 1, pieces[0])
+        for cols, next_cols in zip(pieces, pieces[1:]):
+            gated(last, 0, next_cols)
             add_and_store(last, cols)
+            gated(last, 1, next_cols)
+        add_and_store(last, pieces[-1])

@@ -35,7 +35,10 @@ WORD_GROUP = 2
 SCALE_GROUP = 4
 X_VECTOR_COLUMNS = 9 * N // 16
 H_VECTOR_COLUMNS = 5 * N // 8
-LAST_PASSES = 4
+LAST_PASSES = 5
+HEAD_TILES = STREAMED_TILES // 2
+TAIL_PASSES = 4
+WARM_UP_MATMULS = 10
 LAST_TILE_PIECE = N // 2
 LATE_GROUP = X_PASSES // 2
 CELL_GROUP = 2
@@ -54,8 +57,7 @@ def load_scale_rows(nc, planes, scales, passes, rows, channels):
 
 def load_words(nc, words_sb, words, passes, columns):
     nc.sync.dma_start(
-        out=words_sb[:, passes, :].bitcast(I32),
-        in_=words[passes, :, columns].rearrange("g p b -> p g b").bitcast(I32),
+        out=words_sb.bitcast(I32), in_=words[passes, :, columns].rearrange("g p b -> p g b").bitcast(I32)
     )
 
 
@@ -88,6 +90,7 @@ def tile_mdlstmcellweights_pb_k_kernel(
 
         streamed_words = keep.tile([P, X_PASSES, STREAMED_TILES * TILE_WORD_BYTES], U8, align_bytes=64)
         late_words = keep.tile([P, X_PASSES, LATE_TILES * TILE_WORD_BYTES], U8, align_bytes=64)
+        tail_words = keep.tile([P, TAIL_PASSES, (STREAMED_TILES - HEAD_TILES) * TILE_WORD_BYTES], U8, align_bytes=64)
         streamed_planes = keep.tile([P, X_PASSES, STREAMED_TILES * P], U8, align_bytes=64)
         late_planes = keep.tile([P, X_PASSES, LATE_TILES * P], U8, align_bytes=64)
         ho_words = keep.tile([P, H_PASSES, M_TILES * TILE_WORD_BYTES], U8, align_bytes=64)
@@ -101,9 +104,15 @@ def tile_mdlstmcellweights_pb_k_kernel(
         bias = keep.tile([P, M_TILES], BF16)
         mix = keep.tile([P, DIRS], BF16)
         warm = keep.tile([P, 1], F32)
+        zeros = keep.tile([P, N], BF16)
 
         nc.vector.memset(warm[:], 0.0)
         nc.scalar.activation(out=warm[:], in_=warm[:], func=ACT.Sigmoid)
+
+        nc.vector.memset(zeros[:], 0.0)
+        warm_up = banks.tile([P, N], F32, name="bank")
+        for i in range(WARM_UP_MATMULS):
+            nc.tensor.matmul(out=warm_up[:], lhsT=zeros[:, :P], rhs=zeros[:], start=True, stop=True)
 
         nc.vector.memset(ho_planes[:].rearrange("p g n -> p (g n)").bitcast(I32), 0)
         for g0 in range(0, X_PASSES, SCALE_GROUP):
@@ -117,8 +126,10 @@ def tile_mdlstmcellweights_pb_k_kernel(
             return raw
 
         def load_streamed_words(g):
+            tiles = STREAMED_TILES if g < X_PASSES - TAIL_PASSES else HEAD_TILES
+            columns = slice(0, tiles * TILE_WORD_BYTES)
             passes = slice(g, g + WORD_GROUP)
-            load_words(nc, streamed_words, w_io_words, passes, slice(0, STREAMED_TILES * TILE_WORD_BYTES))
+            load_words(nc, streamed_words[:, passes, columns], w_io_words, passes, columns)
 
         def load_streamed_scales(g, rows):
             load_scale_rows(nc, streamed_planes, w_io_scales, slice(g, g + SCALE_GROUP), rows, STREAMED)
@@ -139,7 +150,8 @@ def tile_mdlstmcellweights_pb_k_kernel(
                     all_rows = range(ROWS_PER_QUADRANT)
                     load_scale_rows(nc, ho_planes, w_ho_scales, slice(0, H_PASSES), all_rows, slice(0, OUT_C))
                 if d == 0:
-                    load_words(nc, ho_words, w_ho_words, slice(c, c + 1), slice(0, M_TILES * TILE_WORD_BYTES))
+                    passes = slice(c, c + 1)
+                    load_words(nc, ho_words[:, passes, :], w_ho_words, passes, slice(0, M_TILES * TILE_WORD_BYTES))
         for g in range(X_PASSES):
             raw_tiles.append(load_pass(x[g * K_PASS : (g + 1) * K_PASS, :]))
             if g == 0:
@@ -150,40 +162,49 @@ def tile_mdlstmcellweights_pb_k_kernel(
             next_group = (g // SCALE_GROUP + 1) * SCALE_GROUP
             if next_group < X_PASSES:
                 load_streamed_scales(next_group, [g % SCALE_GROUP])
-        load_scale_rows(nc, late_planes, w_io_scales, slice(0, X_PASSES), range(ROWS_PER_QUADRANT), LATE)
+        load_words(
+            nc, tail_words[:], w_io_words, slice(X_PASSES - TAIL_PASSES, X_PASSES),
+            slice(HEAD_TILES * TILE_WORD_BYTES, STREAMED_TILES * TILE_WORD_BYTES),
+        )
         load_cell(0, CELL_GROUP)
+        load_scale_rows(nc, late_planes, w_io_scales, slice(0, X_PASSES), range(ROWS_PER_QUADRANT), LATE)
         with nc.allow_non_contiguous_dma(reason="b_o: one 2-byte element for each partition and tile"):
             nc.sync.dma_start(out=bias[:], in_=b_o.rearrange("(m p) o -> p (m o)", p=P))
         nc.sync.dma_start(out=mix[:], in_=weighted_sum.partition_broadcast(P))
         next_cell = CELL_GROUP
         for g0 in range(0, X_PASSES, LATE_GROUP):
-            load_words(
-                nc, late_words, w_io_words, slice(g0, g0 + LATE_GROUP),
-                slice(STREAMED_TILES * TILE_WORD_BYTES, M_TILES * TILE_WORD_BYTES),
-            )
+            passes = slice(g0, g0 + LATE_GROUP)
+            columns = slice(STREAMED_TILES * TILE_WORD_BYTES, M_TILES * TILE_WORD_BYTES)
+            load_words(nc, late_words[:, passes, :], w_io_words, passes, columns)
             load_cell(next_cell, next_cell + CELL_GROUP)
             next_cell += CELL_GROUP
         for m0 in range(next_cell, M_TILES, CELL_GROUP):
             load_cell(m0, m0 + CELL_GROUP)
 
-        def weight_pass(acc, words_sb, planes, g, w, codes, plane, start, stop):
+        def weight_pass(acc, words, scales, codes, plane, start, stop):
             nc.tensor.matmul_mx(
                 out=acc[:],
-                lhsT=words_sb[:, g, w * TILE_WORD_BYTES : (w + 1) * TILE_WORD_BYTES].bitcast(FP4X4),
-                lhsT_scale=planes[:, g, w * P : (w + 1) * P],
+                lhsT=words.bitcast(FP4X4),
+                lhsT_scale=scales,
                 rhs=codes.bitcast(FP8X4),
                 rhs_scale=plane,
                 start=start,
                 stop=stop,
             )
 
+        def word_tile(words_sb, g, w):
+            return words_sb[:, g, w * TILE_WORD_BYTES : (w + 1) * TILE_WORD_BYTES]
+
+        def scale_tile(planes, g, w):
+            return planes[:, g, w * P : (w + 1) * P]
+
         differences = {}
         sums = {}
 
         def h_pass(acc, d, c, m, start, stop):
             weight_pass(
-                acc, ho_words, ho_planes, c, m, h_codes[:, d, c, :], h_planes[:, d, c, :],
-                start=start, stop=stop,
+                acc, word_tile(ho_words, c, m), scale_tile(ho_planes, c, m),
+                h_codes[:, d, c, :], h_planes[:, d, c, :], start=start, stop=stop,
             )
 
         def difference_pass(i, m):
@@ -197,12 +218,18 @@ def tile_mdlstmcellweights_pb_k_kernel(
                 h_pass(sums[m], 1, c, m, start=(c == 0), stop=False)
 
         def x_pass(g, m):
-            if m < STREAMED_TILES:
-                words_sb, planes, w = streamed_words, streamed_planes, m
+            if m >= STREAMED_TILES:
+                words = word_tile(late_words, g, m - STREAMED_TILES)
+                scales = scale_tile(late_planes, g, m - STREAMED_TILES)
             else:
-                words_sb, planes, w = late_words, late_planes, m - STREAMED_TILES
+                in_tail = m >= HEAD_TILES and g >= X_PASSES - TAIL_PASSES
+                if in_tail:
+                    words = word_tile(tail_words, g - (X_PASSES - TAIL_PASSES), m - HEAD_TILES)
+                else:
+                    words = word_tile(streamed_words, g, m)
+                scales = scale_tile(streamed_planes, g, m)
             weight_pass(
-                sums[m], words_sb, planes, g, w, x_codes[:, g, :], x_planes[:, g, :],
+                sums[m], words, scales, x_codes[:, g, :], x_planes[:, g, :],
                 start=False, stop=(g == X_PASSES - 1),
             )
 
@@ -231,6 +258,7 @@ def tile_mdlstmcellweights_pb_k_kernel(
             quantise(i, regroup(raw_tiles[i], H_VECTOR_COLUMNS, negate=(i < H_PASSES)))
             for m in range(M_TILES):
                 difference_pass(i, m)
+        grouped_tiles = [regroup(raw_tiles[DIRS * H_PASSES], X_VECTOR_COLUMNS)]
         for m in range(M_TILES):
             if m % 2 == 0:
                 nc.vector.tensor_copy(out=h_diff[:, m, :], in_=differences[m][:])
@@ -239,9 +267,8 @@ def tile_mdlstmcellweights_pb_k_kernel(
         for m in range(STREAMED_TILES):
             open_sum(m)
 
-        grouped_tiles = []
         for g in range(X_PASSES + 1):
-            if g < X_PASSES:
+            if 0 < g < X_PASSES:
                 grouped_tiles.append(regroup(raw_tiles[DIRS * H_PASSES + g], X_VECTOR_COLUMNS))
             if g > 0:
                 quantise(DIRS * H_PASSES + g - 1, grouped_tiles[g - 1])

@@ -33,7 +33,7 @@ LATE = slice(STREAMED_TILES * P, OUT_C)
 assert LATE_TILES <= PSUM_BANKS - STREAMED_TILES
 WORD_GROUP = 2
 SCALE_GROUP = 4
-X_VECTOR_COLUMNS = 9 * N // 16
+X_VECTOR_COLUMNS = 17 * N // 32
 H_VECTOR_COLUMNS = 5 * N // 8
 LAST_PASSES = 5
 HEAD_TILES = STREAMED_TILES // 2
@@ -162,15 +162,16 @@ def tile_mdlstmcellweights_pb_k_kernel(
             next_group = (g // SCALE_GROUP + 1) * SCALE_GROUP
             if next_group < X_PASSES:
                 load_streamed_scales(next_group, [g % SCALE_GROUP])
+        load_cell(0, 1)
+        with nc.allow_non_contiguous_dma(reason="b_o: one 2-byte element for each partition and tile"):
+            nc.sync.dma_start(out=bias[:], in_=b_o.rearrange("(m p) o -> p (m o)", p=P))
+        nc.sync.dma_start(out=mix[:], in_=weighted_sum.partition_broadcast(P))
         load_words(
             nc, tail_words[:], w_io_words, slice(X_PASSES - TAIL_PASSES, X_PASSES),
             slice(HEAD_TILES * TILE_WORD_BYTES, STREAMED_TILES * TILE_WORD_BYTES),
         )
-        load_cell(0, CELL_GROUP)
+        load_cell(1, CELL_GROUP)
         load_scale_rows(nc, late_planes, w_io_scales, slice(0, X_PASSES), range(ROWS_PER_QUADRANT), LATE)
-        with nc.allow_non_contiguous_dma(reason="b_o: one 2-byte element for each partition and tile"):
-            nc.sync.dma_start(out=bias[:], in_=b_o.rearrange("(m p) o -> p (m o)", p=P))
-        nc.sync.dma_start(out=mix[:], in_=weighted_sum.partition_broadcast(P))
         next_cell = CELL_GROUP
         for g0 in range(0, X_PASSES, LATE_GROUP):
             passes = slice(g0, g0 + LATE_GROUP)
@@ -322,10 +323,10 @@ def tile_mdlstmcellweights_pb_k_kernel(
             sigmoids(m)
             if m + 1 < last:
                 second_sum(m + 1)
-            tanh_cell(m + 1)
-            gated(m, 0)
             if m > 0:
                 add_and_store(m - 1)
+            tanh_cell(m + 1)
+            gated(m, 0)
             gated(m, 1)
         pieces = [slice(c, c + LAST_TILE_PIECE) for c in range(0, N, LAST_TILE_PIECE)]
         second_sum(last, pieces[0])

from contextlib import ExitStack

import concourse.mybir as mybir

F32 = mybir.dt.float32
BF16 = mybir.dt.bfloat16
I32 = mybir.dt.int32
U32 = mybir.dt.uint32
U8 = mybir.dt.uint8
FP8X4 = mybir.dt.float8_e4m3fn_x4
FP4X4 = mybir.dt.float4_e2m1fn_x4
ACT = mybir.ActivationFunctionType
ALU = mybir.AluOpType

P = 128
PACK = 4
K_PASS = P * PACK
IN_C, OUT_C, N = 8192, 1024, 512
X_PASSES = IN_C // K_PASS
H_PASSES = OUT_C // K_PASS
M_TILES = OUT_C // P
DIRS = 2
TILE_WORD_BYTES = P * 2
QUADRANTS = 4
SCALE_ROWS = K_PASS // 32
ROWS_PER_QUADRANT = SCALE_ROWS // QUADRANTS

PSUM_BANKS = 8
STREAMED_TILES = 6
STREAMED = slice(0, STREAMED_TILES * P)
LATE_TILES = M_TILES - STREAMED_TILES
LATE = slice(STREAMED_TILES * P, OUT_C)
assert LATE_TILES <= PSUM_BANKS - STREAMED_TILES
WORD_GROUP = 2
SCALE_GROUP = 4
X_VECTOR_COLUMNS = 17 * N // 32
H_VECTOR_COLUMNS = 5 * N // 8
LAST_PASSES = 5
HEAD_TILES = STREAMED_TILES // 2
TAIL_PASSES = 4
WARM_UP_MATMULS = 10
LAST_TILE_PIECE = N // 2
LATE_GROUP = X_PASSES // 2
CELL_GROUP = 2
RAW_BUFS = 8

FLOPS = 2 * OUT_C * N * (IN_C + DIRS * OUT_C)


def load_scale_rows(nc, planes, scales, passes, rows, channels):
    for r in rows:
        nc.sync.dma_start(
            out=planes[r : P : P // QUADRANTS, passes, :].bitcast(I32),
            in_=scales[passes, r : SCALE_ROWS : ROWS_PER_QUADRANT, channels].rearrange("g q n -> q g n").bitcast(I32),
        )


def load_words(nc, words_sb, words, passes, columns):
    nc.sync.dma_start(
        out=words_sb.bitcast(I32), in_=words[passes, :, columns].rearrange("g p b -> p g b").bitcast(I32)
    )


def tile_mdlstmcellweights_pb_k_kernel(
    tc,
    x,
    h_prev_dim0,
    h_prev_dim1,
    ct0,
    ct1,
    w_io_words,
    w_io_scales,
    w_ho_words,
    w_ho_scales,
    b_o,
    weighted_sum,
    out,
):
    nc = tc.nc
    h_prev = [h_prev_dim0, h_prev_dim1]
    cell = [ct0, ct1]

    with ExitStack() as stack:
        stack.enter_context(tc.manual_schedule())
        keep = stack.enter_context(tc.tile_pool(name="keep", bufs=1))
        raw_pool = stack.enter_context(tc.tile_pool(name="raw", bufs=RAW_BUFS))
        grouped_pool = stack.enter_context(tc.tile_pool(name="grouped", bufs=3))
        work = stack.enter_context(tc.tile_pool(name="work", bufs=4))
        banks = stack.enter_context(tc.psum_pool(name="banks", bufs=PSUM_BANKS))

        streamed_words = keep.tile([P, X_PASSES, STREAMED_TILES * TILE_WORD_BYTES], U8, align_bytes=64)
        late_words = keep.tile([P, X_PASSES, LATE_TILES * TILE_WORD_BYTES], U8, align_bytes=64)
        tail_words = keep.tile([P, TAIL_PASSES, (STREAMED_TILES - HEAD_TILES) * TILE_WORD_BYTES], U8, align_bytes=64)
        streamed_planes = keep.tile([P, X_PASSES, STREAMED_TILES * P], U8, align_bytes=64)
        late_planes = keep.tile([P, X_PASSES, LATE_TILES * P], U8, align_bytes=64)
        ho_words = keep.tile([P, H_PASSES, M_TILES * TILE_WORD_BYTES], U8, align_bytes=64)
        ho_planes = keep.tile([P, H_PASSES, OUT_C], U8, align_bytes=64)
        x_codes = keep.tile([P, X_PASSES, N], U32, align_bytes=64)
        x_planes = keep.tile([P, X_PASSES, N], U8, align_bytes=64)
        h_codes = keep.tile([P, DIRS, H_PASSES, N], U32, align_bytes=64)
        h_planes = keep.tile([P, DIRS, H_PASSES, N], U8, align_bytes=64)
        h_diff = keep.tile([P, M_TILES, N], F32)
        cell_sb = keep.tile([P, M_TILES, DIRS, N], BF16)
        bias = keep.tile([P, M_TILES], BF16)
        mix = keep.tile([P, DIRS], BF16)
        warm = keep.tile([P, 1], F32)
        zeros = keep.tile([P, N], BF16)

        nc.vector.memset(warm[:], 0.0)
        nc.scalar.activation(out=warm[:], in_=warm[:], func=ACT.Sigmoid)

        nc.vector.memset(zeros[:], 0.0)
        warm_up = banks.tile([P, N], F32, name="bank")
        for i in range(WARM_UP_MATMULS):
            nc.tensor.matmul(out=warm_up[:], lhsT=zeros[:, :P], rhs=zeros[:], start=True, stop=True)

        nc.vector.memset(ho_planes[:].rearrange("p g n -> p (g n)").bitcast(I32), 0)
        for g0 in range(0, X_PASSES, SCALE_GROUP):
            group = streamed_planes[:, g0 : g0 + SCALE_GROUP, :]
            nc.vector.memset(group.rearrange("p g n -> p (g n)").bitcast(I32), 0)
        nc.vector.memset(late_planes[:].rearrange("p g n -> p (g n)").bitcast(I32), 0)

        def load_pass(rows):
            raw = raw_pool.tile([P, PACK, N], BF16, name="raw")
            nc.sync.dma_start(out=raw[:], in_=rows.rearrange("(p t) n -> p t n", t=PACK))
            return raw

        def load_streamed_words(g):
            tiles = STREAMED_TILES if g < X_PASSES - TAIL_PASSES else HEAD_TILES
            columns = slice(0, tiles * TILE_WORD_BYTES)
            passes = slice(g, g + WORD_GROUP)
            load_words(nc, streamed_words[:, passes, columns], w_io_words, passes, columns)

        def load_streamed_scales(g, rows):
            load_scale_rows(nc, streamed_planes, w_io_scales, slice(g, g + SCALE_GROUP), rows, STREAMED)

        def load_cell(m0, m1):
            for d in range(DIRS):
                nc.sync.dma_start(
                    out=cell_sb[:, m0:m1, d, :],
                    in_=cell[d][m0 * P : m1 * P, :].rearrange("(m p) n -> p m n", p=P),
                )

        assert SCALE_GROUP == ROWS_PER_QUADRANT
        raw_tiles = []
        for d in range(DIRS):
            for c in range(H_PASSES):
                raw_tiles.append(load_pass(h_prev[d][c * K_PASS : (c + 1) * K_PASS, :]))
                if d == 0 and c == 0:
                    all_rows = range(ROWS_PER_QUADRANT)
                    load_scale_rows(nc, ho_planes, w_ho_scales, slice(0, H_PASSES), all_rows, slice(0, OUT_C))
                if d == 0:
                    passes = slice(c, c + 1)
                    load_words(nc, ho_words[:, passes, :], w_ho_words, passes, slice(0, M_TILES * TILE_WORD_BYTES))
        for g in range(X_PASSES):
            raw_tiles.append(load_pass(x[g * K_PASS : (g + 1) * K_PASS, :]))
            if g == 0:
                load_streamed_scales(0, range(ROWS_PER_QUADRANT))
                load_streamed_words(0)
            if (g + 1) % WORD_GROUP == 0 and g + 1 < X_PASSES:
                load_streamed_words(g + 1)
            next_group = (g // SCALE_GROUP + 1) * SCALE_GROUP
            if next_group < X_PASSES:
                load_streamed_scales(next_group, [g % SCALE_GROUP])
        load_cell(0, 1)
        with nc.allow_non_contiguous_dma(reason="b_o: one 2-byte element for each partition and tile"):
            nc.sync.dma_start(out=bias[:], in_=b_o.rearrange("(m p) o -> p (m o)", p=P))
        nc.sync.dma_start(out=mix[:], in_=weighted_sum.partition_broadcast(P))
        load_words(
            nc, tail_words[:], w_io_words, slice(X_PASSES - TAIL_PASSES, X_PASSES),
            slice(HEAD_TILES * TILE_WORD_BYTES, STREAMED_TILES * TILE_WORD_BYTES),
        )
        load_cell(1, CELL_GROUP)
        load_scale_rows(nc, late_planes, w_io_scales, slice(0, X_PASSES), range(ROWS_PER_QUADRANT), LATE)
        next_cell = CELL_GROUP
        for g0 in range(0, X_PASSES, LATE_GROUP):
            passes = slice(g0, g0 + LATE_GROUP)
            columns = slice(STREAMED_TILES * TILE_WORD_BYTES, M_TILES * TILE_WORD_BYTES)
            load_words(nc, late_words[:, passes, :], w_io_words, passes, columns)
            load_cell(next_cell, next_cell + CELL_GROUP)
            next_cell += CELL_GROUP
        for m0 in range(next_cell, M_TILES, CELL_GROUP):
            load_cell(m0, m0 + CELL_GROUP)

        def weight_pass(acc, words, scales, codes, plane, start, stop):
            nc.tensor.matmul_mx(
                out=acc[:],
                lhsT=words.bitcast(FP4X4),
                lhsT_scale=scales,
                rhs=codes.bitcast(FP8X4),
                rhs_scale=plane,
                start=start,
                stop=stop,
            )

        def word_tile(words_sb, g, w):
            return words_sb[:, g, w * TILE_WORD_BYTES : (w + 1) * TILE_WORD_BYTES]

        def scale_tile(planes, g, w):
            return planes[:, g, w * P : (w + 1) * P]

        differences = {}
        sums = {}

        def h_pass(acc, d, c, m, start, stop):
            weight_pass(
                acc, word_tile(ho_words, c, m), scale_tile(ho_planes, c, m),
                h_codes[:, d, c, :], h_planes[:, d, c, :], start=start, stop=stop,
            )

        def difference_pass(i, m):
            if i == 0:
                differences[m] = banks.tile([P, N], F32, name="bank")
            h_pass(differences[m], i // H_PASSES, i % H_PASSES, m, start=(i == 0), stop=(i == DIRS * H_PASSES - 1))

        def open_sum(m):
            sums[m] = banks.tile([P, N], F32, name="bank")
            for c in range(H_PASSES):
                h_pass(sums[m], 1, c, m, start=(c == 0), stop=False)

        def x_pass(g, m):
            if m >= STREAMED_TILES:
                words = word_tile(late_words, g, m - STREAMED_TILES)
                scales = scale_tile(late_planes, g, m - STREAMED_TILES)
            else:
                in_tail = m >= HEAD_TILES and g >= X_PASSES - TAIL_PASSES
                if in_tail:
                    words = word_tile(tail_words, g - (X_PASSES - TAIL_PASSES), m - HEAD_TILES)
                else:
                    words = word_tile(streamed_words, g, m)
                scales = scale_tile(streamed_planes, g, m)
            weight_pass(
                sums[m], words, scales, x_codes[:, g, :], x_planes[:, g, :],
                start=False, stop=(g == X_PASSES - 1),
            )

        targets = [(h_codes[:, d, c, :], h_planes[:, d, c, :]) for d in range(DIRS) for c in range(H_PASSES)]
        targets.extend([(x_codes[:, g, :], x_planes[:, g, :]) for g in range(X_PASSES)])

        def regroup(raw, split, negate=False):
            grouped = grouped_pool.tile([P, N, PACK], BF16, name="grouped", align_bytes=64)
            vector_out = grouped[:, :split, :].rearrange("p (c i) t -> p c t i", i=4)
            vector_in = raw[:, :, :split].rearrange("p t (c i) -> p c t i", i=4)
            scalar_out = grouped[:, split:, :].rearrange("p (c i) t -> p c t i", i=4)
            scalar_in = raw[:, :, split:].rearrange("p t (c i) -> p c t i", i=4)
            if negate:
                nc.vector.tensor_scalar(out=vector_out, in0=vector_in, scalar1=-1.0, scalar2=None, op0=ALU.mult)
                nc.scalar.activation(out=scalar_out, in_=scalar_in, func=ACT.Copy, scale=-1.0)
            else:
                nc.vector.tensor_copy(out=vector_out, in_=vector_in)
                nc.scalar.copy(out=scalar_out, in_=scalar_in)
            return grouped

        def quantise(i, grouped):
            codes, plane = targets[i]
            nc.vector.quantize_mx(out=codes.bitcast(FP8X4), scales=plane, in_=grouped[:].rearrange("p n t -> p (n t)"))

        for i in range(DIRS * H_PASSES):
            quantise(i, regroup(raw_tiles[i], H_VECTOR_COLUMNS, negate=(i < H_PASSES)))
            for m in range(M_TILES):
                difference_pass(i, m)
        grouped_tiles = [regroup(raw_tiles[DIRS * H_PASSES], X_VECTOR_COLUMNS)]
        for m in range(M_TILES):
            if m % 2 == 0:
                nc.vector.tensor_copy(out=h_diff[:, m, :], in_=differences[m][:])
            else:
                nc.scalar.copy(out=h_diff[:, m, :], in_=differences[m][:])
        for m in range(STREAMED_TILES):
            open_sum(m)

        for g in range(X_PASSES + 1):
            if 0 < g < X_PASSES:
                grouped_tiles.append(regroup(raw_tiles[DIRS * H_PASSES + g], X_VECTOR_COLUMNS))
            if g > 0:
                quantise(DIRS * H_PASSES + g - 1, grouped_tiles[g - 1])
                if g - 1 < X_PASSES - LAST_PASSES:
                    for m in range(STREAMED_TILES):
                        x_pass(g - 1, m)

        for m in range(STREAMED_TILES):
            for g in range(X_PASSES - LAST_PASSES, X_PASSES):
                x_pass(g, m)

        for m in range(STREAMED_TILES, M_TILES):
            open_sum(m)
            for g in range(X_PASSES):
                x_pass(g, m)

        gates, tanhs = {}, {}

        def tanh_cell(m):
            tanhs[m] = work.tile([P, DIRS, N], F32, name="tanh_c")
            nc.scalar.activation(
                out=tanhs[m][:].rearrange("p d n -> p (d n)"),
                in_=cell_sb[:, m, :, :].rearrange("p d n -> p (d n)"),
                func=ACT.Tanh,
            )

        def second_sum(m, cols=slice(0, N)):
            if m not in gates:
                gates[m] = work.tile([P, DIRS, N], F32, name="gate")
            nc.vector.tensor_tensor(out=gates[m][:, 0, cols], in0=sums[m][:, cols], in1=h_diff[:, m, cols], op=ALU.subtract)

        def sigmoids(m, cols=slice(0, N)):
            nc.scalar.activation(out=gates[m][:, 0, cols], in_=gates[m][:, 0, cols], func=ACT.Sigmoid, bias=bias[:, m : m + 1])
            nc.scalar.activation(out=gates[m][:, 1, cols], in_=sums[m][:, cols], func=ACT.Sigmoid, bias=bias[:, m : m + 1])

        def gated(m, d, cols=slice(0, N)):
            nc.vector.scalar_tensor_tensor(
                out=gates[m][:, d, cols], in0=gates[m][:, d, cols], scalar=mix[:, d : d + 1], in1=tanhs[m][:, d, cols],
                op0=ALU.mult, op1=ALU.mult,
            )

        def add_and_store(m, cols=slice(0, N)):
            result = work.tile([P, cols.stop - cols.start], F32, name="result")
            nc.vector.tensor_tensor(out=result[:], in0=gates[m][:, 0, cols], in1=gates[m][:, 1, cols], op=ALU.add)
            nc.sync.dma_start(out=out[m * P : (m + 1) * P, cols], in_=result[:])

        last = M_TILES - 1
        tanh_cell(0)
        second_sum(0)
        for m in range(last):
            sigmoids(m)
            if m + 1 < last:
                second_sum(m + 1)
            if m > 0:
                add_and_store(m - 1)
            tanh_cell(m + 1)
            gated(m, 0)
            gated(m, 1)
        pieces = [slice(c, c + LAST_TILE_PIECE) for c in range(0, N, LAST_TILE_PIECE)]
        second_sum(last, pieces[0])
        add_and_store(last - 1)
        for cols in pieces[1:]:
            second_sum(last, cols)
        for cols in pieces:
            sigmoids(last, cols)
        gated(last, 0, pieces[0])
        gated(last, 1, pieces[0])
        for cols, next_cols in zip(pieces, pieces[1:]):
            gated(last, 0, next_cols)
            add_and_store(last, cols)
            gated(last, 1, next_cols)
        add_and_store(last, pieces[-1])
